import numpy as np
import ml_dtypes


def mxq(x, axis, fmt="e4m3"):
    dtype, down = {"e4m3": (ml_dtypes.float8_e4m3fn, 7), "e5m2": (ml_dtypes.float8_e5m2, 14)}[fmt]
    v = np.moveaxis(np.asarray(x, np.float32).astype(ml_dtypes.bfloat16).astype(np.float64), axis, -1)
    blocks = v.reshape(v.shape[:-1] + (-1, 32))
    amax = np.abs(blocks).max(-1, keepdims=True)
    byte = np.maximum(np.where(amax > 0, np.frexp(amax)[1] - 1 + 127, 0) - down, 1)
    scale = np.exp2(byte - 127.0)
    codes = (blocks / scale).astype(np.float32).astype(dtype).astype(np.float64)
    return np.moveaxis((codes * scale).reshape(v.shape), -1, axis)


WIDE = False


def mx_kscale(k):
    if not WIDE:
        return np.ones(k)
    levels = np.array([10, -10, 5, -5, 0])
    if k % 512:
        return np.exp2(np.random.permutation(np.resize(levels, k // 32))).repeat(32)
    a = np.empty((k // 512, 16))
    for p in range(k // 512):
        a[p, :8] = np.random.permutation(np.resize(levels, 8))
        for g in range(8):
            far = levels[np.abs(levels - a[p, g]) >= 10]
            a[p, g + 8] = far[np.random.randint(len(far))]
    return np.exp2(a.ravel()).repeat(32)


BF16 = ml_dtypes.bfloat16


def bf(x):
    return np.asarray(x, np.float32).astype(BF16)


def f64(x):
    return np.asarray(x).astype(np.float64)


B, S, D, QR, KR, H, NOPE, ROPE, VD = 2, 256, 2048, 1536, 512, 16, 128, 64, 128
EPS = 1e-6
THETA = 10000.0
LAT = 3.0 * np.sqrt(EPS)


def rmsnorm(x, w):
    var = np.mean(x * x, axis=-1, keepdims=True)
    return w * (x * (1.0 / np.sqrt(var + EPS)))


def rope_cos_sin(seq_len):
    inv_freq = 1.0 / (THETA ** (f64(np.arange(0, ROPE, 2)) / ROPE))
    t = f64(np.arange(seq_len))
    freqs = np.outer(t, inv_freq)
    emb = np.concatenate([freqs, freqs], -1)
    return np.cos(emb), np.sin(emb)


def rotate_half(x):
    x1, x2 = x[..., : x.shape[-1] // 2], x[..., x.shape[-1] // 2 :]
    return np.concatenate([-x2, x1], axis=-1)


def setup_inputs():
    s, t = mx_kscale(D), mx_kscale(KR)
    return {"hidden_states": bf(np.random.standard_normal((B, S, D)) * s),
            "kv_a_w_ckv": bf(np.random.standard_normal((KR, D)) * LAT / np.sqrt(D) / s[None, :]),
            "k_pe_raw": bf(np.random.standard_normal((B, S, ROPE))),
            "kv_a_ln_w": bf((1.0 + 0.1 * np.random.standard_normal(KR)) * t),
            "kv_b_w": bf(np.random.standard_normal((H * (NOPE + VD), KR)) / np.sqrt(KR) / t[None, :])}


def reference(hidden_states, kv_a_w_ckv, k_pe_raw, kv_a_ln_w, kv_b_w):
    ckv = mxq(f64(hidden_states), 2, "e4m3") @ mxq(f64(kv_a_w_ckv), 1, "e4m3").T
    ckv_n = rmsnorm(ckv, f64(kv_a_ln_w))
    kv = mxq(ckv_n, 2, "e4m3") @ mxq(f64(kv_b_w), 1, "e4m3").T
    kv = kv.reshape(B, S, H, NOPE + VD).transpose(0, 2, 1, 3)
    k_nope, v = kv[..., :NOPE], kv[..., NOPE:]
    k_pe = f64(k_pe_raw).reshape(B, 1, S, ROPE)
    cos, sin = rope_cos_sin(S)
    cos, sin = cos[None, None], sin[None, None]
    k_pe = k_pe * cos + rotate_half(k_pe) * sin
    key_s = np.concatenate([k_nope, np.broadcast_to(k_pe, (B, H, S, ROPE))], -1)
    return key_s, v

@@ -1,0 +1,484 @@
+import math
+from contextlib import ExitStack
+
+import concourse.mybir as mybir
+from concourse.masks import make_identity
+
+F32 = mybir.dt.float32
+BF16 = mybir.dt.bfloat16
+I32 = mybir.dt.int32
+U32 = mybir.dt.uint32
+U8 = mybir.dt.uint8
+FP8X4 = mybir.dt.float8_e4m3fn_x4
+ALU = mybir.AluOpType
+ACT = mybir.ActivationFunctionType
+
+P = 128
+BATCH = 2
+D_MODEL = 2048
+LATENT = 512
+HEADS = 16
+NOPE = 128
+ROPE = 64
+K_PASS = 512
+PASSES = D_MODEL // K_PASS
+BANK = 512
+TILES = 4
+PAIRS = HEADS // 2
+SPLIT_PAIRS = 3
+EPS = 1e-6
+THETA = 10000.0
+WARM_START = 9
+FLOPS = 2 * BATCH * 256 * D_MODEL * LATENT + 2 * BATCH * 256 * LATENT * HEADS * 2 * NOPE
+
+
+def tile_modelnew_pb_kernel(
+    tc, hidden_states, kv_a_w_ckv, k_pe_raw, kv_a_ln_w, kv_b_w, out_0, out_1
+):
+    nc = tc.nc
+    with ExitStack() as ctx:
+        ctx.enter_context(tc.manual_schedule())
+        const = ctx.enter_context(tc.tile_pool(name="const", bufs=1))
+        raw = ctx.enter_context(tc.tile_pool(name="raw", bufs=1))
+        keep = ctx.enter_context(tc.tile_pool(name="keep", bufs=1))
+        outs = ctx.enter_context(tc.tile_pool(name="outs", bufs=1))
+        grp = ctx.enter_context(tc.tile_pool(name="grp", bufs=4))
+        work = ctx.enter_context(tc.tile_pool(name="work", bufs=TILES))
+        psum = ctx.enter_context(tc.psum_pool(name="psum", bufs=8))
+
+        kpe = const.tile([P, TILES, ROPE], BF16)
+        for b in range(BATCH):
+            nc.scalar.dma_start(
+                out=kpe[b:P:BATCH, :, :],
+                in_=k_pe_raw[b].rearrange("(q j) d -> q j d", j=TILES),
+            )
+        ones = const.tile([P, P], BF16)
+        nc.vector.memset(ones[:], 1.0)
+        zeros = const.tile([P, BANK], BF16)
+        nc.vector.memset(zeros[:], 0.0)
+        gain_row = const.tile([P, LATENT], BF16)
+        nc.vector.memset(gain_row[:], 0.0)
+        nc.scalar.dma_start(
+            out=gain_row[0:1, :], in_=kv_a_ln_w.rearrange("(o n) -> o n", o=1)
+        )
+
+        loaded = {}
+        wa_view = kv_a_w_ckv.rearrange("(p t) k -> t p k", t=4)
+        for t in range(4):
+            wa_raw = raw.tile([P, D_MODEL], BF16, name="wa_raw%d" % t)
+            nc.sync.dma_start(out=wa_raw[:], in_=wa_view[t])
+            loaded[("wa", t)] = wa_raw
+        x_view = hidden_states.rearrange("b (q j) k -> b j q k", j=TILES)
+        for j in range(TILES):
+            x_raw = raw.tile([P, D_MODEL], BF16, name="x_raw%d" % j)
+            for b in range(BATCH):
+                nc.sync.dma_start(out=x_raw[b:P:BATCH, :], in_=x_view[b, j])
+            loaded[("x", j)] = x_raw
+        wb_view = kv_b_w.rearrange("(c p i) k -> c p (i k)", c=PAIRS, i=4)
+        for c in range(PAIRS):
+            wb_raw = raw.tile([P, 4 * LATENT], BF16, name="wb_raw%d" % c)
+            nc.sync.dma_start(out=wb_raw[:], in_=wb_view[c])
+            loaded[("wb", c)] = wb_raw
+
+        twice_p = const.tile([P, TILES], I32)
+        nc.gpsimd.iota(out=twice_p[:], pattern=[[0, TILES]], base=0, channel_multiplier=2)
+        j_index = const.tile([P, TILES], I32)
+        nc.gpsimd.iota(out=j_index[:], pattern=[[1, TILES]], base=0, channel_multiplier=0)
+        ident_f32 = const.tile([P, P], F32)
+        make_identity(nc, ident_f32[:])
+        ident_bf16 = const.tile([P, P], BF16)
+        make_identity(nc, ident_bf16[:])
+        eps = const.tile([P, 1], F32)
+        nc.vector.memset(eps[:], EPS)
+        zero = const.tile([P, 1], F32)
+        nc.vector.memset(zero[:], 0.0)
+
+        sin_first = const.tile([P, 1], F32)
+        nc.scalar.activation(out=sin_first[:], in_=zero[:], func=ACT.Sin)
+
+        four_q = const.tile([P, TILES], I32)
+        nc.vector.tensor_single_scalar(
+            out=four_q[:], in_=twice_p[:], scalar=0x1FC, op=ALU.bitwise_and
+        )
+        position = const.tile([P, TILES], F32)
+        nc.vector.tensor_tensor(
+            out=position[:], in0=four_q[:], in1=j_index[:], op=ALU.add
+        )
+        turns = const.tile([P, 2, TILES, ROPE // 2], F32)
+        nc.vector.tensor_scalar(
+            out=turns[:, 0, :, 0:1],
+            in0=position[:].unsqueeze(2),
+            scalar1=1.0 / (2.0 * math.pi),
+            scalar2=None,
+            op0=ALU.mult,
+        )
+        ratio = THETA ** (-2.0 / ROPE)
+        for w in (1, 2, 4, 8, 16):
+            nc.vector.tensor_scalar(
+                out=turns[:, 0, :, w : 2 * w],
+                in0=turns[:, 0, :, 0:w],
+                scalar1=ratio**w,
+                scalar2=None,
+                op0=ALU.mult,
+            )
+        nc.vector.tensor_scalar(
+            out=turns[:, 1], in0=turns[:, 0], scalar1=0.25, scalar2=None, op0=ALU.add
+        )
+        n_table = 2 * TILES * (ROPE // 2)
+        turns_flat = turns[:].rearrange("p c j f -> p (c j f)")
+        whole_i32 = const.tile([P, n_table], I32)
+        nc.vector.tensor_copy(out=whole_i32[:], in_=turns_flat)
+        whole = const.tile([P, n_table], F32)
+        nc.vector.tensor_copy(out=whole[:], in_=whole_i32[:])
+        remainder = const.tile([P, n_table], F32)
+        nc.vector.tensor_tensor(
+            out=remainder[:], in0=turns_flat, in1=whole[:], op=ALU.subtract
+        )
+        less_turns = const.tile([P, n_table], F32)
+        nc.vector.scalar_tensor_tensor(
+            out=less_turns[:],
+            in0=remainder[:],
+            scalar=0.5,
+            in1=remainder[:],
+            op0=ALU.is_gt,
+            op1=ALU.subtract,
+        )
+        sin_cos = const.tile([P, 2, TILES, ROPE // 2], F32)
+        nc.scalar.activation(
+            out=sin_cos[:].rearrange("p c j f -> p (c j f)"),
+            in_=less_turns[:],
+            func=ACT.Sin,
+            scale=-2.0 * math.pi,
+        )
+        sqrt_early = const.tile([P, 1], F32)
+        nc.scalar.activation(out=sqrt_early[:], in_=eps[:], func=ACT.Sqrt)
+
+        half = ROPE // 2
+        sin = sin_cos[:, 0]
+        cos = sin_cos[:, 1]
+        by_cos = const.tile([P, TILES, ROPE], F32)
+        nc.vector.tensor_tensor(
+            out=by_cos[:].rearrange("p j (h f) -> p j h f", h=2),
+            in0=kpe[:].rearrange("p j (h f) -> p j h f", h=2),
+            in1=cos.unsqueeze(2).to_broadcast([P, TILES, 2, half]),
+            op=ALU.mult,
+        )
+        by_sin = const.tile([P, TILES, ROPE], F32)
+        nc.vector.scalar_tensor_tensor(
+            out=by_sin[:, :, 0:half],
+            in0=kpe[:, :, half:ROPE],
+            scalar=-1.0,
+            in1=sin,
+            op0=ALU.mult,
+            op1=ALU.mult,
+        )
+        nc.vector.tensor_tensor(
+            out=by_sin[:, :, half:ROPE], in0=kpe[:, :, 0:half], in1=sin, op=ALU.mult
+        )
+        rotated = const.tile([P, TILES, ROPE], F32)
+        nc.vector.tensor_tensor(
+            out=rotated[:], in0=by_cos[:], in1=by_sin[:], op=ALU.add
+        )
+
+        wa_codes = keep.tile([P, PASSES, LATENT], U32, align_bytes=64)
+        wa_scales = keep.tile([P, PASSES, LATENT], U8, align_bytes=64)
+        x_codes = keep.tile([P, TILES, PASSES, P], U32, align_bytes=64)
+        x_scales = keep.tile([P, TILES, PASSES, P], U8, align_bytes=64)
+        n_codes = keep.tile([P, TILES, P], U32, align_bytes=64)
+        n_scales = keep.tile([P, TILES, P], U8, align_bytes=64)
+        wb_codes = keep.tile([P, PAIRS, BANK], U32, align_bytes=64)
+        wb_scales = keep.tile([P, PAIRS, BANK], U8, align_bytes=64)
+
+        gain_all = const.tile([P, LATENT], F32)
+        key_view = out_0.rearrange("b h (q j) d -> b q h j d", j=TILES)
+        value_view = out_1.rearrange("b h (q j) d -> b q h j d", j=TILES)
+
+        live = {}
+
+        def on_vector(out, in_):
+            nc.vector.tensor_copy(out=out, in_=in_)
+
+        def on_scalar(out, in_):
+            nc.scalar.copy(out=out, in_=in_)
+
+        def keep_clock_up(count):
+            if "dummy" not in live:
+                dummy = psum.tile([P, BANK], F32, tag="bank")
+                live["dummy"] = dummy
+            for repeat in range(count):
+                nc.tensor.matmul(
+                    out=live["dummy"][:], lhsT=ones[:], rhs=zeros[:], start=True, stop=True
+                )
+
+        def spread_gain():
+            gain_bank = psum.tile([P, LATENT], F32, tag="bank")
+            nc.tensor.matmul(
+                out=gain_bank[:], lhsT=ones[:], rhs=gain_row[:], start=True, stop=True
+            )
+            live["gain"] = gain_bank
+
+        def order_gain():
+            nc.vector.tensor_copy(
+                out=gain_all[:].rearrange("q (t p) -> q t p", t=4),
+                in_=live["gain"][:].rearrange("q (p t) -> q t p", t=4),
+            )
+
+        def transpose_pairs(what, index):
+            pairs = loaded[(what, index)][:].bitcast(F32)
+            for h in range(2):
+                bank = psum.tile([P, BANK], F32, tag="bank")
+                for m in range(4):
+                    run, u = 2 * h + m // 2, m % 2
+                    nc.tensor.transpose(
+                        out=bank[:, m * P : (m + 1) * P],
+                        in_=pairs[:, 2 * P * run + u : 2 * P * (run + 1) : 2],
+                        identity=ident_f32[:],
+                    )
+                live[("bank", what, index, h)] = bank
+
+        def grouped_tile(what, index):
+            if ("grouped", what, index) not in live:
+                grouped = grp.tile([P, 4 * BANK], BF16, tag="grouped", align_bytes=64)
+                live[("grouped", what, index)] = grouped
+            return live[("grouped", what, index)]
+
+        def regroup(what, index, h, copy):
+            view = (
+                grouped_tile(what, index)[:]
+                .bitcast(F32)
+                .rearrange("q (g r u) -> q g r u", g=PASSES, u=2)
+            )
+            copy(
+                view[:, 2 * h : 2 * h + 2],
+                live[("bank", what, index, h)][:].rearrange("q (g u r) -> q g r u", g=2, u=2),
+            )
+
+        def regroup_rows(c, copy):
+            view = (
+                grouped_tile("wb", c)[:]
+                .bitcast(F32)
+                .rearrange("q (p a m) -> q a p m", a=2, m=4)
+            )
+            for a in range(2):
+                copy(view[:, a], live[("bank", "wb", c, a)][:].rearrange("q (m p) -> q p m", m=4))
+
+        def quantise(what, index):
+            grouped = live[("grouped", what, index)]
+            if what == "wa":
+                rows = slice(index * P, (index + 1) * P)
+                for g in range(PASSES):
+                    nc.vector.quantize_mx(
+                        out=wa_codes[:, g, rows].bitcast(FP8X4),
+                        scales=wa_scales[:, g, rows],
+                        in_=grouped[:, g * 4 * P : (g + 1) * 4 * P],
+                    )
+            elif what == "x":
+                nc.vector.quantize_mx(
+                    out=x_codes[:, index].rearrange("q g r -> q (g r)").bitcast(FP8X4),
+                    scales=x_scales[:, index].rearrange("q g r -> q (g r)"),
+                    in_=grouped[:],
+                )
+            else:
+                nc.vector.quantize_mx(
+                    out=wb_codes[:, index, :].bitcast(FP8X4),
+                    scales=wb_scales[:, index, :],
+                    in_=grouped[:],
+                )
+
+        def first_matmul(j):
+            ckv = psum.tile([P, LATENT], F32, tag="bank")
+            for g in range(PASSES):
+                nc.tensor.matmul_mx(
+                    out=ckv[:],
+                    lhsT=x_codes[:, j, g, :].bitcast(FP8X4),
+                    lhsT_scale=x_scales[:, j, g, :],
+                    rhs=wa_codes[:, g, :].bitcast(FP8X4),
+                    rhs_scale=wa_scales[:, g, :],
+                    start=(g == 0),
+                    stop=(g == PASSES - 1),
+                )
+            live[("ckv", j)] = ckv
+
+        def root_mean_square(j):
+            squares = work.tile([P, LATENT], BF16, tag="squares")
+            sum_squares = work.tile([P, 1], F32, tag="sum_squares")
+            nc.scalar.activation(
+                out=squares[:], in_=live[("ckv", j)][:], func=ACT.Square, accum_out=sum_squares[:]
+            )
+            rms = work.tile([P, 1], F32, tag="rms")
+            nc.scalar.activation(
+                out=rms[:], in_=sum_squares[:], func=ACT.Sqrt, bias=eps[:], scale=1.0 / LATENT
+            )
+            live[("rms", j)] = rms
+
+        def normalise(j):
+            inverse = work.tile([P, 1], F32, tag="inverse")
+            nc.vector.reciprocal(out=inverse[:], in_=live[("rms", j)][:])
+            normed = work.tile([P, LATENT], BF16, tag="normed")
+            nc.vector.scalar_tensor_tensor(
+                out=normed[:],
+                in0=live[("ckv", j)][:],
+                scalar=inverse[:],
+                in1=gain_all[:],
+                op0=ALU.mult,
+                op1=ALU.mult,
+            )
+            live[("normed", j)] = normed
+
+        def transpose_normed(j):
+            bank = psum.tile([P, 4, P], BF16, tag="bank")
+            for t in range(4):
+                nc.tensor.transpose(
+                    out=bank[:, t, :],
+                    in_=live[("normed", j)][:, t * P : (t + 1) * P],
+                    identity=ident_bf16[:],
+                )
+            live[("bank", "normed", j)] = bank
+
+        def regroup_normed(j, copy):
+            grouped = work.tile([P, P, 4], BF16, tag="grouped_normed", align_bytes=64)
+            copy(grouped[:], live[("bank", "normed", j)][:].rearrange("q t r -> q r t"))
+            live[("grouped", "normed", j)] = grouped
+
+        def quantise_normed(j):
+            nc.vector.quantize_mx(
+                out=n_codes[:, j, :].bitcast(FP8X4),
+                scales=n_scales[:, j, :],
+                in_=live[("grouped", "normed", j)][:].rearrange("q r t -> q (r t)"),
+            )
+
+        def fill_rotated(c):
+            key = outs.tile([P, 2, TILES, NOPE + ROPE], F32, name="key%d" % c)
+            value = outs.tile([P, 2, TILES, NOPE], F32, name="value%d" % c)
+            live[("key", c)] = key
+            live[("value", c)] = value
+            nc.vector.tensor_copy(
+                out=key[:, :, :, NOPE : NOPE + ROPE],
+                in_=rotated[:].unsqueeze(1).to_broadcast([P, 2, TILES, ROPE]),
+            )
+
+        def second_matmul(c, j):
+            kv = psum.tile([P, BANK], F32, tag="bank")
+            nc.tensor.matmul_mx(
+                out=kv[:],
+                lhsT=n_codes[:, j, :].bitcast(FP8X4),
+                lhsT_scale=n_scales[:, j, :],
+                rhs=wb_codes[:, c, :].bitcast(FP8X4),
+                rhs_scale=wb_scales[:, c, :],
+                start=True,
+                stop=True,
+            )
+            live[("kv", c, j)] = kv
+
+        def copy_out(c, j, copy):
+            parts = live[("kv", c, j)][:].rearrange("p (h s d) -> p h s d", h=2, s=2)
+            copy(live[("key", c)][:, :, j, 0:NOPE], parts[:, :, 0, :])
+            copy(live[("value", c)][:, :, j, :], parts[:, :, 1, :])
+
+        def store(c, j0, j1):
+            heads = slice(2 * c, 2 * c + 2)
+            for b in range(BATCH):
+                nc.sync.dma_start(
+                    out=key_view[b, :, heads, j0:j1, :],
+                    in_=live[("key", c)][b:P:BATCH, :, j0:j1, :],
+                )
+                nc.sync.dma_start(
+                    out=value_view[b, :, heads, j0:j1, :],
+                    in_=live[("value", c)][b:P:BATCH, :, j0:j1, :],
+                )
+
+        keep_clock_up(WARM_START)
+        for c in range(SPLIT_PAIRS):
+            fill_rotated(c)
+        arrivals = (
+            ("wa", 0), ("wa", 1), ("wa", 2), ("wa", 3), ("x", 0), ("x", 1), ("x", 2), ("x", 3),
+        )
+        for n, (what, index) in enumerate(arrivals):
+            transpose_pairs(what, index)
+            keep_clock_up(1)
+            if n == 1:
+                spread_gain()
+            regroup(what, index, 0, on_scalar)
+            regroup(what, index, 1, on_vector if n % 2 == 0 else on_scalar)
+            if n > 0:
+                quantise(*arrivals[n - 1])
+            if n == 1:
+                order_gain()
+
+        first_matmul(0)
+        quantise("x", 3)
+        first_matmul(1)
+        root_mean_square(0)
+        transpose_pairs("wb", 0)
+        root_mean_square(1)
+        normalise(0)
+        transpose_pairs("wb", 1)
+        regroup_rows(0, on_vector)
+        transpose_normed(0)
+        first_matmul(2)
+        regroup_rows(1, on_scalar)
+        normalise(1)
+        quantise("wb", 0)
+        regroup_normed(0, on_scalar)
+        transpose_normed(1)
+        transpose_pairs("wb", 2)
+        root_mean_square(2)
+        quantise("wb", 1)
+        regroup_normed(1, on_vector)
+        first_matmul(3)
+        regroup_rows(2, on_scalar)
+        quantise_normed(0)
+        quantise_normed(1)
+        normalise(2)
+        second_matmul(0, 0)
+        second_matmul(0, 1)
+        root_mean_square(3)
+        quantise("wb", 2)
+        second_matmul(1, 0)
+        second_matmul(1, 1)
+        transpose_normed(2)
+        copy_out(0, 0, on_vector)
+        copy_out(0, 1, on_scalar)
+        store(0, 0, 2)
+        normalise(3)
+        second_matmul(2, 0)
+        second_matmul(2, 1)
+        copy_out(1, 1, on_scalar)
+        copy_out(1, 0, on_vector)
+        store(1, 0, 2)
+        regroup_normed(2, on_scalar)
+        transpose_normed(3)
+        transpose_pairs("wb", 3)
+        quantise_normed(2)
+        copy_out(2, 0, on_scalar)
+        copy_out(2, 1, on_scalar)
+        store(2, 0, 2)
+        regroup_normed(3, on_vector)
+        quantise_normed(3)
+        for c in range(SPLIT_PAIRS):
+            second_matmul(c, 2)
+            second_matmul(c, 3)
+        regroup_rows(3, on_vector)
+        copy_out(0, 2, on_scalar)
+        copy_out(0, 3, on_scalar)
+        store(0, 2, 4)
+        copy_out(1, 3, on_vector)
+        copy_out(1, 2, on_scalar)
+        store(1, 2, 4)
+        quantise("wb", 3)
+        copy_out(2, 3, on_scalar)
+        copy_out(2, 2, on_vector)
+        store(2, 2, 4)
+
+        for c in range(SPLIT_PAIRS, PAIRS):
+            if c + 1 < PAIRS:
+                transpose_pairs("wb", c + 1)
+                regroup_rows(c + 1, on_scalar)
+            fill_rotated(c)
+            for j in range(TILES):
+                second_matmul(c, j)
+            for j in range(TILES):
+                copy_out(c, j, on_vector if j % 2 == 0 else on_scalar)
+            store(c, 0, TILES)
+            if c + 1 < PAIRS:
+                quantise("wb", c + 1)

@@ -25,7 +25,8 @@ PASSES = D_MODEL // K_PASS
 BANK = 512
 TILES = 4
 PAIRS = HEADS // 2
-SPLIT_PAIRS = 3
+KEY_TILES = 4
+SPLIT_PAIRS = 2
 EPS = 1e-6
 THETA = 10000.0
 WARM_START = 9
@@ -43,6 +44,7 @@ def tile_modelnew_pb_kernel(
         keep = ctx.enter_context(tc.tile_pool(name="keep", bufs=1))
         outs = ctx.enter_context(tc.tile_pool(name="outs", bufs=1))
         grp = ctx.enter_context(tc.tile_pool(name="grp", bufs=4))
+        wa_grp = ctx.enter_context(tc.tile_pool(name="wa_grp", bufs=2))
         work = ctx.enter_context(tc.tile_pool(name="work", bufs=TILES))
         psum = ctx.enter_context(tc.psum_pool(name="psum", bufs=8))
 
@@ -55,133 +57,110 @@ def tile_modelnew_pb_kernel(
         ones = const.tile([P, P], BF16)
         nc.vector.memset(ones[:], 1.0)
         zeros = const.tile([P, BANK], BF16)
-        nc.vector.memset(zeros[:], 0.0)
-        gain_row = const.tile([P, LATENT], BF16)
-        nc.vector.memset(gain_row[:], 0.0)
-        nc.scalar.dma_start(
-            out=gain_row[0:1, :], in_=kv_a_ln_w.rearrange("(o n) -> o n", o=1)
-        )
-
-        loaded = {}
-        wa_view = kv_a_w_ckv.rearrange("(p t) k -> t p k", t=4)
-        for t in range(4):
-            wa_raw = raw.tile([P, D_MODEL], BF16, name="wa_raw%d" % t)
-            nc.sync.dma_start(out=wa_raw[:], in_=wa_view[t])
-            loaded[("wa", t)] = wa_raw
-        x_view = hidden_states.rearrange("b (q j) k -> b j q k", j=TILES)
-        for j in range(TILES):
-            x_raw = raw.tile([P, D_MODEL], BF16, name="x_raw%d" % j)
-            for b in range(BATCH):
-                nc.sync.dma_start(out=x_raw[b:P:BATCH, :], in_=x_view[b, j])
-            loaded[("x", j)] = x_raw
-        wb_view = kv_b_w.rearrange("(c p i) k -> c p (i k)", c=PAIRS, i=4)
-        for c in range(PAIRS):
-            wb_raw = raw.tile([P, 4 * LATENT], BF16, name="wb_raw%d" % c)
-            nc.sync.dma_start(out=wb_raw[:], in_=wb_view[c])
-            loaded[("wb", c)] = wb_raw
-
+        nc.vector.memset(zeros[:].bitcast(F32), 0.0)
         twice_p = const.tile([P, TILES], I32)
         nc.gpsimd.iota(out=twice_p[:], pattern=[[0, TILES]], base=0, channel_multiplier=2)
         j_index = const.tile([P, TILES], I32)
         nc.gpsimd.iota(out=j_index[:], pattern=[[1, TILES]], base=0, channel_multiplier=0)
+        gain_row = const.tile([P, LATENT], BF16)
+        nc.gpsimd.memset(gain_row[:].bitcast(F32), 0.0)
+        sin_first = const.tile([P, 1], F32)
+        nc.scalar.activation(out=sin_first[:], in_=ones[:, 0:1], func=ACT.Sin)
+
+        loaded = {}
+        wa_view = kv_a_w_ckv.rearrange("(p t) k -> t p k", t=4)
+        x_view = hidden_states.rearrange("b (q j) k -> b j q k", j=TILES)
+        wb_view = kv_b_w.rearrange("(c p i) k -> c p (i k)", c=PAIRS, i=4)
+
+        def load(what, index):
+            tile = raw.tile([P, D_MODEL], BF16, name="%s_raw%d" % (what, index))
+            if what == "wa":
+                nc.sync.dma_start(out=tile[:], in_=wa_view[index])
+            elif what == "x":
+                for b in range(BATCH):
+                    nc.sync.dma_start(out=tile[b:P:BATCH, :], in_=x_view[b, index])
+            else:
+                nc.sync.dma_start(out=tile[:], in_=wb_view[index])
+            loaded[(what, index)] = tile
+
+        for t in range(4):
+            load("wa", t)
+        load("x", 0)
+        load("x", 1)
+        load("wb", 0)
+        load("x", 2)
+        load("x", 3)
+        for c in range(1, PAIRS):
+            load("wb", c)
+
         ident_f32 = const.tile([P, P], F32)
         make_identity(nc, ident_f32[:])
         ident_bf16 = const.tile([P, P], BF16)
         make_identity(nc, ident_bf16[:])
         eps = const.tile([P, 1], F32)
-        nc.vector.memset(eps[:], EPS)
-        zero = const.tile([P, 1], F32)
-        nc.vector.memset(zero[:], 0.0)
-
-        sin_first = const.tile([P, 1], F32)
-        nc.scalar.activation(out=sin_first[:], in_=zero[:], func=ACT.Sin)
-
-        four_q = const.tile([P, TILES], I32)
-        nc.vector.tensor_single_scalar(
-            out=four_q[:], in_=twice_p[:], scalar=0x1FC, op=ALU.bitwise_and
+        nc.gpsimd.memset(eps[:], EPS)
+        nc.gpsimd.dma_start(
+            out=gain_row[0:1, :], in_=kv_a_ln_w.rearrange("(o n) -> o n", o=1)
         )
-        position = const.tile([P, TILES], F32)
-        nc.vector.tensor_tensor(
-            out=position[:], in0=four_q[:], in1=j_index[:], op=ALU.add
-        )
-        turns = const.tile([P, 2, TILES, ROPE // 2], F32)
+
+        half = ROPE // 2
+        ratio = THETA ** (-2.0 / ROPE)
+        freq = const.tile([P, half], F32)
         nc.vector.tensor_scalar(
-            out=turns[:, 0, :, 0:1],
-            in0=position[:].unsqueeze(2),
+            out=freq[:, 0:1],
+            in0=ones[:, 0:1],
             scalar1=1.0 / (2.0 * math.pi),
             scalar2=None,
             op0=ALU.mult,
         )
-        ratio = THETA ** (-2.0 / ROPE)
-        for w in (1, 2, 4, 8, 16):
-            nc.vector.tensor_scalar(
-                out=turns[:, 0, :, w : 2 * w],
-                in0=turns[:, 0, :, 0:w],
-                scalar1=ratio**w,
-                scalar2=None,
-                op0=ALU.mult,
-            )
+        four_q = const.tile([P, TILES], I32)
+        nc.vector.tensor_single_scalar(
+            out=four_q[:], in_=twice_p[:], scalar=0x1FC, op=ALU.bitwise_and
+        )
+        for width, copies in ((1, 4), (4, 4), (16, 2)):
+            for r in range(1, copies):
+                nc.vector.tensor_scalar(
+                    out=freq[:, r * width : (r + 1) * width],
+                    in0=freq[:, 0:width],
+                    scalar1=ratio ** (r * width),
+                    scalar2=None,
+                    op0=ALU.mult,
+                )
+        position = const.tile([P, TILES], F32)
+        nc.vector.tensor_tensor(
+            out=position[:], in0=four_q[:], in1=j_index[:], op=ALU.add
+        )
+        turns = const.tile([P, 2, TILES, half], F32)
+        nc.vector.tensor_tensor(
+            out=turns[:, 0],
+            in0=position[:].unsqueeze(2).to_broadcast([P, TILES, half]),
+            in1=freq[:].unsqueeze(1).to_broadcast([P, TILES, half]),
+            op=ALU.mult,
+        )
         nc.vector.tensor_scalar(
             out=turns[:, 1], in0=turns[:, 0], scalar1=0.25, scalar2=None, op0=ALU.add
         )
-        n_table = 2 * TILES * (ROPE // 2)
+        n_table = 2 * TILES * half
         turns_flat = turns[:].rearrange("p c j f -> p (c j f)")
-        whole_i32 = const.tile([P, n_table], I32)
-        nc.vector.tensor_copy(out=whole_i32[:], in_=turns_flat)
-        whole = const.tile([P, n_table], F32)
-        nc.vector.tensor_copy(out=whole[:], in_=whole_i32[:])
+        whole = const.tile([P, n_table], I32)
+        nc.vector.tensor_copy(out=whole[:], in_=turns_flat)
         remainder = const.tile([P, n_table], F32)
         nc.vector.tensor_tensor(
             out=remainder[:], in0=turns_flat, in1=whole[:], op=ALU.subtract
         )
-        less_turns = const.tile([P, n_table], F32)
-        nc.vector.scalar_tensor_tensor(
-            out=less_turns[:],
-            in0=remainder[:],
-            scalar=0.5,
-            in1=remainder[:],
-            op0=ALU.is_gt,
-            op1=ALU.subtract,
-        )
         sin_cos = const.tile([P, 2, TILES, ROPE // 2], F32)
         nc.scalar.activation(
             out=sin_cos[:].rearrange("p c j f -> p (c j f)"),
-            in_=less_turns[:],
+            in_=remainder[:],
             func=ACT.Sin,
-            scale=-2.0 * math.pi,
+            scale=2.0 * math.pi,
         )
+
         sqrt_early = const.tile([P, 1], F32)
         nc.scalar.activation(out=sqrt_early[:], in_=eps[:], func=ACT.Sqrt)
 
-        half = ROPE // 2
-        sin = sin_cos[:, 0]
-        cos = sin_cos[:, 1]
-        by_cos = const.tile([P, TILES, ROPE], F32)
-        nc.vector.tensor_tensor(
-            out=by_cos[:].rearrange("p j (h f) -> p j h f", h=2),
-            in0=kpe[:].rearrange("p j (h f) -> p j h f", h=2),
-            in1=cos.unsqueeze(2).to_broadcast([P, TILES, 2, half]),
-            op=ALU.mult,
-        )
-        by_sin = const.tile([P, TILES, ROPE], F32)
-        nc.vector.scalar_tensor_tensor(
-            out=by_sin[:, :, 0:half],
-            in0=kpe[:, :, half:ROPE],
-            scalar=-1.0,
-            in1=sin,
-            op0=ALU.mult,
-            op1=ALU.mult,
-        )
-        nc.vector.tensor_tensor(
-            out=by_sin[:, :, half:ROPE], in0=kpe[:, :, 0:half], in1=sin, op=ALU.mult
-        )
-        rotated = const.tile([P, TILES, ROPE], F32)
-        nc.vector.tensor_tensor(
-            out=rotated[:], in0=by_cos[:], in1=by_sin[:], op=ALU.add
-        )
-
-        wa_codes = keep.tile([P, PASSES, LATENT], U32, align_bytes=64)
-        wa_scales = keep.tile([P, PASSES, LATENT], U8, align_bytes=64)
+        wa_codes = keep.tile([P, 2, PASSES, 2 * P], U32, align_bytes=64)
+        wa_scales = keep.tile([P, 2, PASSES, 2 * P], U8, align_bytes=64)
         x_codes = keep.tile([P, TILES, PASSES, P], U32, align_bytes=64)
         x_scales = keep.tile([P, TILES, PASSES, P], U8, align_bytes=64)
         n_codes = keep.tile([P, TILES, P], U32, align_bytes=64)
@@ -218,7 +197,7 @@ def tile_modelnew_pb_kernel(
             live["gain"] = gain_bank
 
         def order_gain():
-            nc.vector.tensor_copy(
+            nc.scalar.copy(
                 out=gain_all[:].rearrange("q (t p) -> q t p", t=4),
                 in_=live["gain"][:].rearrange("q (p t) -> q t p", t=4),
             )
@@ -238,16 +217,23 @@ def tile_modelnew_pb_kernel(
 
         def grouped_tile(what, index):
             if ("grouped", what, index) not in live:
-                grouped = grp.tile([P, 4 * BANK], BF16, tag="grouped", align_bytes=64)
+                if what == "wa":
+                    grouped = wa_grp.tile([P, 8 * BANK], BF16, tag="grouped_wa", align_bytes=64)
+                else:
+                    grouped = grp.tile([P, 4 * BANK], BF16, tag="grouped", align_bytes=64)
                 live[("grouped", what, index)] = grouped
             return live[("grouped", what, index)]
 
         def regroup(what, index, h, copy):
+            if what == "wa":
+                rows = slice((index % 2) * P, (index % 2 + 1) * P)
+                grouped = grouped_tile(what, index // 2)
+            else:
+                rows = slice(0, P)
+                grouped = grouped_tile(what, index)
             view = (
-                grouped_tile(what, index)[:]
-                .bitcast(F32)
-                .rearrange("q (g r u) -> q g r u", g=PASSES, u=2)
-            )
+                grouped[:].bitcast(F32).rearrange("q (g r u) -> q g r u", g=PASSES, u=2)
+            )[:, :, rows, :]
             copy(
                 view[:, 2 * h : 2 * h + 2],
                 live[("bank", what, index, h)][:].rearrange("q (g u r) -> q g r u", g=2, u=2),
@@ -262,16 +248,22 @@ def tile_modelnew_pb_kernel(
             for a in range(2):
                 copy(view[:, a], live[("bank", "wb", c, a)][:].rearrange("q (m p) -> q p m", m=4))
 
+        def regroup_bank(c, a, copy):
+            view = (
+                grouped_tile("wb", c)[:]
+                .bitcast(F32)
+                .rearrange("q (p a m) -> q a p m", a=2, m=4)
+            )
+            copy(view[:, a], live[("bank", "wb", c, a)][:].rearrange("q (m p) -> q p m", m=4))
+
         def quantise(what, index):
             grouped = live[("grouped", what, index)]
             if what == "wa":
-                rows = slice(index * P, (index + 1) * P)
-                for g in range(PASSES):
-                    nc.vector.quantize_mx(
-                        out=wa_codes[:, g, rows].bitcast(FP8X4),
-                        scales=wa_scales[:, g, rows],
-                        in_=grouped[:, g * 4 * P : (g + 1) * 4 * P],
-                    )
+                nc.vector.quantize_mx(
+                    out=wa_codes[:, index].rearrange("q g r -> q (g r)").bitcast(FP8X4),
+                    scales=wa_scales[:, index].rearrange("q g r -> q (g r)"),
+                    in_=grouped[:],
+                )
             elif what == "x":
                 nc.vector.quantize_mx(
                     out=x_codes[:, index].rearrange("q g r -> q (g r)").bitcast(FP8X4),
@@ -287,16 +279,17 @@ def tile_modelnew_pb_kernel(
 
         def first_matmul(j):
             ckv = psum.tile([P, LATENT], F32, tag="bank")
-            for g in range(PASSES):
-                nc.tensor.matmul_mx(
-                    out=ckv[:],
-                    lhsT=x_codes[:, j, g, :].bitcast(FP8X4),
-                    lhsT_scale=x_scales[:, j, g, :],
-                    rhs=wa_codes[:, g, :].bitcast(FP8X4),
-                    rhs_scale=wa_scales[:, g, :],
-                    start=(g == 0),
-                    stop=(g == PASSES - 1),
-                )
+            for half in range(2):
+                for g in range(PASSES):
+                    nc.tensor.matmul_mx(
+                        out=ckv[:, half * 2 * P : (half + 1) * 2 * P],
+                        lhsT=x_codes[:, j, g, :].bitcast(FP8X4),
+                        lhsT_scale=x_scales[:, j, g, :],
+                        rhs=wa_codes[:, half, g, :].bitcast(FP8X4),
+                        rhs_scale=wa_scales[:, half, g, :],
+                        start=(g == 0),
+                        stop=(g == PASSES - 1),
+                    )
             live[("ckv", j)] = ckv
 
         def root_mean_square(j):
@@ -311,14 +304,17 @@ def tile_modelnew_pb_kernel(
             )
             live[("rms", j)] = rms
 
-        def normalise(j):
+        def invert(j):
             inverse = work.tile([P, 1], F32, tag="inverse")
             nc.vector.reciprocal(out=inverse[:], in_=live[("rms", j)][:])
+            live[("inverse", j)] = inverse
+
+        def normalise(j):
             normed = work.tile([P, LATENT], BF16, tag="normed")
             nc.vector.scalar_tensor_tensor(
                 out=normed[:],
                 in0=live[("ckv", j)][:],
-                scalar=inverse[:],
+                scalar=live[("inverse", j)][:],
                 in1=gain_all[:],
                 op0=ALU.mult,
                 op1=ALU.mult,
@@ -347,15 +343,44 @@ def tile_modelnew_pb_kernel(
                 in_=live[("grouped", "normed", j)][:].rearrange("q r t -> q (r t)"),
             )
 
+        def rotate():
+            sin = sin_cos[:, 0]
+            cos = sin_cos[:, 1]
+            by_cos = const.tile([P, TILES, ROPE], F32)
+            nc.vector.tensor_tensor(
+                out=by_cos[:].rearrange("p j (h f) -> p j h f", h=2),
+                in0=kpe[:].rearrange("p j (h f) -> p j h f", h=2),
+                in1=cos.unsqueeze(2).to_broadcast([P, TILES, 2, half]),
+                op=ALU.mult,
+            )
+            by_sin = const.tile([P, TILES, ROPE], F32)
+            nc.vector.scalar_tensor_tensor(
+                out=by_sin[:, :, 0:half],
+                in0=kpe[:, :, half:ROPE],
+                scalar=-1.0,
+                in1=sin,
+                op0=ALU.mult,
+                op1=ALU.mult,
+            )
+            nc.vector.tensor_tensor(
+                out=by_sin[:, :, half:ROPE], in0=kpe[:, :, 0:half], in1=sin, op=ALU.mult
+            )
+            rotated = const.tile([P, TILES, ROPE], F32)
+            nc.vector.tensor_tensor(
+                out=rotated[:], in0=by_cos[:], in1=by_sin[:], op=ALU.add
+            )
+            live["rotated"] = rotated
+
         def fill_rotated(c):
             key = outs.tile([P, 2, TILES, NOPE + ROPE], F32, name="key%d" % c)
-            value = outs.tile([P, 2, TILES, NOPE], F32, name="value%d" % c)
-            live[("key", c)] = key
-            live[("value", c)] = value
             nc.vector.tensor_copy(
                 out=key[:, :, :, NOPE : NOPE + ROPE],
-                in_=rotated[:].unsqueeze(1).to_broadcast([P, 2, TILES, ROPE]),
+                in_=live["rotated"][:].unsqueeze(1).to_broadcast([P, 2, TILES, ROPE]),
             )
+            for pair in range(c, PAIRS, KEY_TILES):
+                live[("key", pair)] = key
+                value = outs.tile([P, 2, TILES, NOPE], F32, name="value%d" % pair)
+                live[("value", pair)] = value
 
         def second_matmul(c, j):
             kv = psum.tile([P, BANK], F32, tag="bank")
@@ -387,98 +412,123 @@ def tile_modelnew_pb_kernel(
                     in_=live[("value", c)][b:P:BATCH, :, j0:j1, :],
                 )
 
-        keep_clock_up(WARM_START)
-        for c in range(SPLIT_PAIRS):
-            fill_rotated(c)
-        arrivals = (
-            ("wa", 0), ("wa", 1), ("wa", 2), ("wa", 3), ("x", 0), ("x", 1), ("x", 2), ("x", 3),
-        )
-        for n, (what, index) in enumerate(arrivals):
-            transpose_pairs(what, index)
-            keep_clock_up(1)
-            if n == 1:
-                spread_gain()
-            regroup(what, index, 0, on_scalar)
-            regroup(what, index, 1, on_vector if n % 2 == 0 else on_scalar)
-            if n > 0:
-                quantise(*arrivals[n - 1])
-            if n == 1:
-                order_gain()
-
+        keep_clock_up(4)
+        transpose_pairs("wa", 0)
+        regroup("wa", 0, 0, on_scalar)
+        regroup("wa", 0, 1, on_vector)
+        keep_clock_up(1)
+        transpose_pairs("wa", 1)
+        regroup("wa", 1, 0, on_scalar)
+        regroup("wa", 1, 1, on_vector)
+        transpose_pairs("wa", 2)
+        regroup("wa", 2, 0, on_scalar)
+        rotate()
+        keep_clock_up(1)
+        regroup("wa", 2, 1, on_scalar)
+        quantise("wa", 0)
+        transpose_pairs("wa", 3)
+        regroup("wa", 3, 0, on_scalar)
+        regroup("wa", 3, 1, on_vector)
+        keep_clock_up(1)
+        fill_rotated(0)
+        transpose_pairs("x", 0)
+        regroup("x", 0, 0, on_scalar)
+        quantise("wa", 1)
+        keep_clock_up(1)
+        regroup("x", 0, 1, on_scalar)
+        quantise("x", 0)
+        transpose_pairs("x", 1)
+        regroup("x", 1, 0, on_scalar)
+        transpose_pairs("wb", 0)
+        regroup("x", 1, 1, on_scalar)
+        quantise("x", 1)
+        spread_gain()
+        order_gain()
+        regroup_bank(0, 0, on_vector)
         first_matmul(0)
-        quantise("x", 3)
+        regroup_bank(0, 1, on_scalar)
+        quantise("wb", 0)
         first_matmul(1)
         root_mean_square(0)
-        transpose_pairs("wb", 0)
+        invert(0)
+        transpose_pairs("x", 2)
         root_mean_square(1)
+        fill_rotated(1)
+        regroup("x", 2, 0, on_scalar)
         normalise(0)
-        transpose_pairs("wb", 1)
-        regroup_rows(0, on_vector)
         transpose_normed(0)
-        first_matmul(2)
-        regroup_rows(1, on_scalar)
-        normalise(1)
-        quantise("wb", 0)
         regroup_normed(0, on_scalar)
+        regroup("x", 2, 1, on_vector)
+        transpose_pairs("x", 3)
+        regroup("x", 3, 0, on_scalar)
+        invert(1)
+        fill_rotated(2)
+        normalise(1)
         transpose_normed(1)
-        transpose_pairs("wb", 2)
-        root_mean_square(2)
-        quantise("wb", 1)
-        regroup_normed(1, on_vector)
-        first_matmul(3)
-        regroup_rows(2, on_scalar)
+        regroup_normed(1, on_scalar)
         quantise_normed(0)
-        quantise_normed(1)
-        normalise(2)
+        transpose_pairs("wb", 1)
+        quantise("x", 2)
         second_matmul(0, 0)
+        copy_out(0, 0, on_scalar)
+        regroup("x", 3, 1, on_vector)
+        first_matmul(2)
+        regroup_bank(1, 0, on_scalar)
+        quantise_normed(1)
         second_matmul(0, 1)
+        root_mean_square(2)
+        quantise("x", 3)
+        first_matmul(3)
         root_mean_square(3)
-        quantise("wb", 2)
-        second_matmul(1, 0)
-        second_matmul(1, 1)
-        transpose_normed(2)
-        copy_out(0, 0, on_vector)
-        copy_out(0, 1, on_scalar)
+        regroup_bank(1, 1, on_vector)
+        transpose_pairs("wb", 2)
+        regroup_bank(2, 0, on_scalar)
+        copy_out(0, 1, on_vector)
         store(0, 0, 2)
-        normalise(3)
-        second_matmul(2, 0)
-        second_matmul(2, 1)
-        copy_out(1, 1, on_scalar)
-        copy_out(1, 0, on_vector)
-        store(1, 0, 2)
+        invert(2)
+        quantise("wb", 1)
+        second_matmul(1, 0)
+        copy_out(1, 0, on_scalar)
+        normalise(2)
+        second_matmul(1, 1)
+        invert(3)
+        transpose_normed(2)
         regroup_normed(2, on_scalar)
+        copy_out(1, 1, on_vector)
+        store(1, 0, 2)
+        regroup_bank(2, 1, on_scalar)
+        normalise(3)
         transpose_normed(3)
-        transpose_pairs("wb", 3)
+        regroup_normed(3, on_scalar)
         quantise_normed(2)
-        copy_out(2, 0, on_scalar)
-        copy_out(2, 1, on_scalar)
-        store(2, 0, 2)
-        regroup_normed(3, on_vector)
-        quantise_normed(3)
-        for c in range(SPLIT_PAIRS):
-            second_matmul(c, 2)
-            second_matmul(c, 3)
-        regroup_rows(3, on_vector)
+        second_matmul(0, 2)
         copy_out(0, 2, on_scalar)
+        quantise("wb", 2)
+        second_matmul(1, 2)
+        quantise_normed(3)
+        second_matmul(0, 3)
         copy_out(0, 3, on_scalar)
         store(0, 2, 4)
+        fill_rotated(3)
+        second_matmul(1, 3)
+        copy_out(1, 2, on_vector)
+        transpose_pairs("wb", 3)
+        regroup_bank(3, 0, on_scalar)
         copy_out(1, 3, on_vector)
-        copy_out(1, 2, on_scalar)
         store(1, 2, 4)
-        quantise("wb", 3)
-        copy_out(2, 3, on_scalar)
-        copy_out(2, 2, on_vector)
-        store(2, 2, 4)
+        regroup_bank(3, 1, on_scalar)
 
         for c in range(SPLIT_PAIRS, PAIRS):
-            if c + 1 < PAIRS:
-                transpose_pairs("wb", c + 1)
-                regroup_rows(c + 1, on_scalar)
-            fill_rotated(c)
             for j in range(TILES):
                 second_matmul(c, j)
-            for j in range(TILES):
-                copy_out(c, j, on_vector if j % 2 == 0 else on_scalar)
-            store(c, 0, TILES)
+            if c + 2 < PAIRS:
+                transpose_pairs("wb", c + 2)
+            copy_out(c, 0, on_vector)
+            copy_out(c, 1, on_scalar)
             if c + 1 < PAIRS:
                 quantise("wb", c + 1)
+            copy_out(c, 2, on_vector)
+            copy_out(c, 3, on_scalar)
+            store(c, 0, TILES)
+            if c + 2 < PAIRS:
+                regroup_rows(c + 2, on_scalar)

@@ -25,7 +25,9 @@ PASSES = D_MODEL // K_PASS
 BANK = 512
 TILES = 4
 PAIRS = HEADS // 2
-KEY_TILES = 4
+OUT_TILES = 4
+HEAD_KEY = TILES * (NOPE + ROPE)
+HEAD_OUT = 2 * HEAD_KEY
 SPLIT_PAIRS = 2
 EPS = 1e-6
 THETA = 10000.0
@@ -372,14 +374,18 @@ def tile_modelnew_pb_kernel(
             live["rotated"] = rotated
 
         def fill_rotated(c):
-            key = outs.tile([P, 2, TILES, NOPE + ROPE], F32, name="key%d" % c)
+            last = (TILES - 1) * (NOPE + ROPE)
+            both = outs.tile([P, 2 * HEAD_OUT + last], F32, name="out%d" % c)
+            heads = both[:, 0 : 2 * HEAD_OUT].rearrange("p (h y) -> p h y", h=2)
+            key = heads[:, :, 0:HEAD_KEY].rearrange("p h (j d) -> p h j d", j=TILES)
+            value = heads[:, :, HEAD_KEY : HEAD_KEY + TILES * NOPE].rearrange("p h (j d) -> p h j d", j=TILES)
             nc.vector.tensor_copy(
                 out=key[:, :, :, NOPE : NOPE + ROPE],
                 in_=live["rotated"][:].unsqueeze(1).to_broadcast([P, 2, TILES, ROPE]),
             )
-            for pair in range(c, PAIRS, KEY_TILES):
+            for pair in range(c, PAIRS, OUT_TILES):
+                live[("both", pair)] = both
                 live[("key", pair)] = key
-                value = outs.tile([P, 2, TILES, NOPE], F32, name="value%d" % pair)
                 live[("value", pair)] = value
 
         def second_matmul(c, j):
@@ -397,8 +403,12 @@ def tile_modelnew_pb_kernel(
 
         def copy_out(c, j, copy):
             parts = live[("kv", c, j)][:].rearrange("p (h s d) -> p h s d", h=2, s=2)
-            copy(live[("key", c)][:, :, j, 0:NOPE], parts[:, :, 0, :])
-            copy(live[("value", c)][:, :, j, :], parts[:, :, 1, :])
+            first = j * (NOPE + ROPE)
+            apart = HEAD_KEY + j * NOPE - first
+            view = live[("both", c)][:, first : first + 2 * HEAD_OUT]
+            view = view.rearrange("p (h y) -> p h y", h=2)[:, :, 0 : 2 * apart]
+            view = view.rearrange("p h (s x) -> p h s x", s=2)[:, :, :, 0:NOPE]
+            copy(view, parts)
 
         def store(c, j0, j1):
             heads = slice(2 * c, 2 * c + 2)

@@ -56,6 +56,11 @@ def tile_modelnew_pb_kernel(
                 out=kpe[b:P:BATCH, :, :],
                 in_=k_pe_raw[b].rearrange("(q j) d -> q j d", j=TILES),
             )
+        gain_row = const.tile([P, LATENT], BF16)
+        nc.vector.memset(gain_row[:].bitcast(F32), 0.0)
+        nc.scalar.dma_start(
+            out=gain_row[0:1, :], in_=kv_a_ln_w.rearrange("(o n) -> o n", o=1)
+        )
         ones = const.tile([P, P], BF16)
         nc.vector.memset(ones[:], 1.0)
         zeros = const.tile([P, BANK], BF16)
@@ -64,8 +69,6 @@ def tile_modelnew_pb_kernel(
         nc.gpsimd.iota(out=twice_p[:], pattern=[[0, TILES]], base=0, channel_multiplier=2)
         j_index = const.tile([P, TILES], I32)
         nc.gpsimd.iota(out=j_index[:], pattern=[[1, TILES]], base=0, channel_multiplier=0)
-        gain_row = const.tile([P, LATENT], BF16)
-        nc.gpsimd.memset(gain_row[:].bitcast(F32), 0.0)
         sin_first = const.tile([P, 1], F32)
         nc.scalar.activation(out=sin_first[:], in_=ones[:, 0:1], func=ACT.Sin)
 
@@ -87,12 +90,9 @@ def tile_modelnew_pb_kernel(
 
         for t in range(4):
             load("wa", t)
-        load("x", 0)
-        load("x", 1)
-        load("wb", 0)
-        load("x", 2)
-        load("x", 3)
-        for c in range(1, PAIRS):
+        for j in range(TILES):
+            load("x", j)
+        for c in range(PAIRS):
             load("wb", c)
 
         ident_f32 = const.tile([P, P], F32)
@@ -101,9 +101,6 @@ def tile_modelnew_pb_kernel(
         make_identity(nc, ident_bf16[:])
         eps = const.tile([P, 1], F32)
         nc.gpsimd.memset(eps[:], EPS)
-        nc.gpsimd.dma_start(
-            out=gain_row[0:1, :], in_=kv_a_ln_w.rearrange("(o n) -> o n", o=1)
-        )
 
         half = ROPE // 2
         ratio = THETA ** (-2.0 / ROPE)
@@ -182,13 +179,13 @@ def tile_modelnew_pb_kernel(
         def on_scalar(out, in_):
             nc.scalar.copy(out=out, in_=in_)
 
-        def keep_clock_up(count):
+        def keep_clock_up(count, columns=BANK):
             if "dummy" not in live:
                 dummy = psum.tile([P, BANK], F32, tag="bank")
                 live["dummy"] = dummy
             for repeat in range(count):
                 nc.tensor.matmul(
-                    out=live["dummy"][:], lhsT=ones[:], rhs=zeros[:], start=True, stop=True
+                    out=live["dummy"][:, 0:columns], lhsT=ones[:], rhs=zeros[:, 0:columns], start=True, stop=True
                 )
 
         def spread_gain():
@@ -199,7 +196,7 @@ def tile_modelnew_pb_kernel(
             live["gain"] = gain_bank
 
         def order_gain():
-            nc.scalar.copy(
+            nc.vector.tensor_copy(
                 out=gain_all[:].rearrange("q (t p) -> q t p", t=4),
                 in_=live["gain"][:].rearrange("q (p t) -> q t p", t=4),
             )
@@ -422,113 +419,84 @@ def tile_modelnew_pb_kernel(
                     in_=live[("value", c)][b:P:BATCH, :, j0:j1, :],
                 )
 
-        keep_clock_up(4)
+        keep_clock_up(3)
+        spread_gain()
+        order_gain()
         transpose_pairs("wa", 0)
-        regroup("wa", 0, 0, on_scalar)
+        regroup("wa", 0, 0, on_vector)
         regroup("wa", 0, 1, on_vector)
-        keep_clock_up(1)
         transpose_pairs("wa", 1)
         regroup("wa", 1, 0, on_scalar)
         regroup("wa", 1, 1, on_vector)
         transpose_pairs("wa", 2)
         regroup("wa", 2, 0, on_scalar)
-        rotate()
-        keep_clock_up(1)
-        regroup("wa", 2, 1, on_scalar)
         quantise("wa", 0)
+        regroup("wa", 2, 1, on_scalar)
         transpose_pairs("wa", 3)
         regroup("wa", 3, 0, on_scalar)
         regroup("wa", 3, 1, on_vector)
-        keep_clock_up(1)
-        fill_rotated(0)
         transpose_pairs("x", 0)
         regroup("x", 0, 0, on_scalar)
         quantise("wa", 1)
-        keep_clock_up(1)
         regroup("x", 0, 1, on_scalar)
-        quantise("x", 0)
         transpose_pairs("x", 1)
+        quantise("x", 0)
         regroup("x", 1, 0, on_scalar)
-        transpose_pairs("wb", 0)
         regroup("x", 1, 1, on_scalar)
-        quantise("x", 1)
-        spread_gain()
-        order_gain()
-        regroup_bank(0, 0, on_vector)
-        first_matmul(0)
-        regroup_bank(0, 1, on_scalar)
-        quantise("wb", 0)
-        first_matmul(1)
-        root_mean_square(0)
-        invert(0)
         transpose_pairs("x", 2)
-        root_mean_square(1)
-        fill_rotated(1)
+        quantise("x", 1)
         regroup("x", 2, 0, on_scalar)
-        normalise(0)
-        transpose_normed(0)
-        regroup_normed(0, on_scalar)
         regroup("x", 2, 1, on_vector)
         transpose_pairs("x", 3)
         regroup("x", 3, 0, on_scalar)
-        invert(1)
-        fill_rotated(2)
-        normalise(1)
+        quantise("x", 2)
+        regroup("x", 3, 1, on_scalar)
+        quantise("x", 3)
+        for j in range(TILES):
+            first_matmul(j)
+        rotate()
+        fill_rotated(0)
+        for j in range(TILES):
+            root_mean_square(j)
+            invert(j)
+            normalise(j)
+        transpose_normed(0)
         transpose_normed(1)
+        regroup_normed(0, on_scalar)
+        transpose_pairs("wb", 0)
         regroup_normed(1, on_scalar)
         quantise_normed(0)
-        transpose_pairs("wb", 1)
-        quantise("x", 2)
-        second_matmul(0, 0)
-        copy_out(0, 0, on_scalar)
-        regroup("x", 3, 1, on_vector)
-        first_matmul(2)
-        regroup_bank(1, 0, on_scalar)
-        quantise_normed(1)
-        second_matmul(0, 1)
-        root_mean_square(2)
-        quantise("x", 3)
-        first_matmul(3)
-        root_mean_square(3)
-        regroup_bank(1, 1, on_vector)
-        transpose_pairs("wb", 2)
-        regroup_bank(2, 0, on_scalar)
-        copy_out(0, 1, on_vector)
-        store(0, 0, 2)
-        invert(2)
-        quantise("wb", 1)
-        second_matmul(1, 0)
-        copy_out(1, 0, on_scalar)
-        normalise(2)
-        second_matmul(1, 1)
-        invert(3)
         transpose_normed(2)
-        regroup_normed(2, on_scalar)
-        copy_out(1, 1, on_vector)
-        store(1, 0, 2)
-        regroup_bank(2, 1, on_scalar)
-        normalise(3)
         transpose_normed(3)
+        regroup_bank(0, 0, on_scalar)
+        quantise_normed(1)
+        regroup_bank(0, 1, on_vector)
+        regroup_normed(2, on_scalar)
+        transpose_pairs("wb", 1)
+        quantise("wb", 0)
         regroup_normed(3, on_scalar)
         quantise_normed(2)
-        second_matmul(0, 2)
-        copy_out(0, 2, on_scalar)
-        quantise("wb", 2)
-        second_matmul(1, 2)
+        second_matmul(0, 0)
+        second_matmul(0, 1)
         quantise_normed(3)
+        regroup_bank(1, 0, on_scalar)
+        copy_out(0, 0, on_vector)
+        second_matmul(0, 2)
         second_matmul(0, 3)
-        copy_out(0, 3, on_scalar)
+        copy_out(0, 1, on_scalar)
+        store(0, 0, 2)
+        regroup_bank(1, 1, on_vector)
+        copy_out(0, 2, on_scalar)
+        copy_out(0, 3, on_vector)
         store(0, 2, 4)
+        quantise("wb", 1)
+        fill_rotated(1)
+        transpose_pairs("wb", 2)
+        regroup_rows(2, on_scalar)
+        fill_rotated(2)
         fill_rotated(3)
-        second_matmul(1, 3)
-        copy_out(1, 2, on_vector)
-        transpose_pairs("wb", 3)
-        regroup_bank(3, 0, on_scalar)
-        copy_out(1, 3, on_vector)
-        store(1, 2, 4)
-        regroup_bank(3, 1, on_scalar)
 
-        for c in range(SPLIT_PAIRS, PAIRS):
+        for c in range(1, PAIRS):
             for j in range(TILES):
                 second_matmul(c, j)
             if c + 2 < PAIRS:

@@ -56,11 +56,6 @@ def tile_modelnew_pb_kernel(
                 out=kpe[b:P:BATCH, :, :],
                 in_=k_pe_raw[b].rearrange("(q j) d -> q j d", j=TILES),
             )
-        gain_row = const.tile([P, LATENT], BF16)
-        nc.vector.memset(gain_row[:].bitcast(F32), 0.0)
-        nc.scalar.dma_start(
-            out=gain_row[0:1, :], in_=kv_a_ln_w.rearrange("(o n) -> o n", o=1)
-        )
         ones = const.tile([P, P], BF16)
         nc.vector.memset(ones[:], 1.0)
         zeros = const.tile([P, BANK], BF16)
@@ -69,6 +64,8 @@ def tile_modelnew_pb_kernel(
         nc.gpsimd.iota(out=twice_p[:], pattern=[[0, TILES]], base=0, channel_multiplier=2)
         j_index = const.tile([P, TILES], I32)
         nc.gpsimd.iota(out=j_index[:], pattern=[[1, TILES]], base=0, channel_multiplier=0)
+        gain_row = const.tile([P, LATENT], BF16)
+        nc.gpsimd.memset(gain_row[:].bitcast(F32), 0.0)
         sin_first = const.tile([P, 1], F32)
         nc.scalar.activation(out=sin_first[:], in_=ones[:, 0:1], func=ACT.Sin)
 
@@ -101,6 +98,9 @@ def tile_modelnew_pb_kernel(
         make_identity(nc, ident_bf16[:])
         eps = const.tile([P, 1], F32)
         nc.gpsimd.memset(eps[:], EPS)
+        nc.gpsimd.dma_start(
+            out=gain_row[0:1, :], in_=kv_a_ln_w.rearrange("(o n) -> o n", o=1)
+        )
 
         half = ROPE // 2
         ratio = THETA ** (-2.0 / ROPE)
@@ -196,7 +196,7 @@ def tile_modelnew_pb_kernel(
             live["gain"] = gain_bank
 
         def order_gain():
-            nc.vector.tensor_copy(
+            nc.scalar.copy(
                 out=gain_all[:].rearrange("q (t p) -> q t p", t=4),
                 in_=live["gain"][:].rearrange("q (p t) -> q t p", t=4),
             )
@@ -419,9 +419,7 @@ def tile_modelnew_pb_kernel(
                     in_=live[("value", c)][b:P:BATCH, :, j0:j1, :],
                 )
 
-        keep_clock_up(3)
-        spread_gain()
-        order_gain()
+        keep_clock_up(4)
         transpose_pairs("wa", 0)
         regroup("wa", 0, 0, on_vector)
         regroup("wa", 0, 1, on_vector)
@@ -451,6 +449,8 @@ def tile_modelnew_pb_kernel(
         regroup("x", 3, 0, on_scalar)
         quantise("x", 2)
         regroup("x", 3, 1, on_scalar)
+        spread_gain()
+        order_gain()
         quantise("x", 3)
         for j in range(TILES):
             first_matmul(j)

@@ -46,6 +46,7 @@ def tile_modelnew_pb_kernel(
         keep = ctx.enter_context(tc.tile_pool(name="keep", bufs=1))
         outs = ctx.enter_context(tc.tile_pool(name="outs", bufs=1))
         grp = ctx.enter_context(tc.tile_pool(name="grp", bufs=4))
+        sep = ctx.enter_context(tc.tile_pool(name="sep", bufs=3))
         wa_grp = ctx.enter_context(tc.tile_pool(name="wa_grp", bufs=2))
         work = ctx.enter_context(tc.tile_pool(name="work", bufs=TILES))
         psum = ctx.enter_context(tc.psum_pool(name="psum", bufs=8))
@@ -56,6 +57,11 @@ def tile_modelnew_pb_kernel(
                 out=kpe[b:P:BATCH, :, :],
                 in_=k_pe_raw[b].rearrange("(q j) d -> q j d", j=TILES),
             )
+        gain_row = const.tile([P, LATENT], BF16)
+        nc.vector.memset(gain_row[:].bitcast(F32), 0.0)
+        nc.scalar.dma_start(
+            out=gain_row[0:1, :], in_=kv_a_ln_w.rearrange("(o n) -> o n", o=1)
+        )
         ones = const.tile([P, P], BF16)
         nc.vector.memset(ones[:], 1.0)
         zeros = const.tile([P, BANK], BF16)
@@ -64,8 +70,6 @@ def tile_modelnew_pb_kernel(
         nc.gpsimd.iota(out=twice_p[:], pattern=[[0, TILES]], base=0, channel_multiplier=2)
         j_index = const.tile([P, TILES], I32)
         nc.gpsimd.iota(out=j_index[:], pattern=[[1, TILES]], base=0, channel_multiplier=0)
-        gain_row = const.tile([P, LATENT], BF16)
-        nc.gpsimd.memset(gain_row[:].bitcast(F32), 0.0)
         sin_first = const.tile([P, 1], F32)
         nc.scalar.activation(out=sin_first[:], in_=ones[:, 0:1], func=ACT.Sin)
 
@@ -98,9 +102,6 @@ def tile_modelnew_pb_kernel(
         make_identity(nc, ident_bf16[:])
         eps = const.tile([P, 1], F32)
         nc.gpsimd.memset(eps[:], EPS)
-        nc.gpsimd.dma_start(
-            out=gain_row[0:1, :], in_=kv_a_ln_w.rearrange("(o n) -> o n", o=1)
-        )
 
         half = ROPE // 2
         ratio = THETA ** (-2.0 / ROPE)
@@ -156,7 +157,7 @@ def tile_modelnew_pb_kernel(
         )
 
         sqrt_early = const.tile([P, 1], F32)
-        nc.scalar.activation(out=sqrt_early[:], in_=eps[:], func=ACT.Sqrt)
+        nc.scalar.activation(out=sqrt_early[:], in_=eps[:], func=ACT.Abs_reciprocal_sqrt)
 
         wa_codes = keep.tile([P, 2, PASSES, 2 * P], U32, align_bytes=64)
         wa_scales = keep.tile([P, 2, PASSES, 2 * P], U8, align_bytes=64)
@@ -196,10 +197,18 @@ def tile_modelnew_pb_kernel(
             live["gain"] = gain_bank
 
         def order_gain():
-            nc.scalar.copy(
+            nc.vector.tensor_copy(
                 out=gain_all[:].rearrange("q (t p) -> q t p", t=4),
                 in_=live["gain"][:].rearrange("q (p t) -> q t p", t=4),
             )
+
+        def separate(what, index):
+            apart = sep.tile([P, 4, 2, P], F32, tag="apart")
+            nc.vector.tensor_copy(
+                out=apart[:],
+                in_=loaded[(what, index)][:].bitcast(F32).rearrange("p (n q u) -> p n u q", n=4, u=2),
+            )
+            live[("apart", what, index)] = apart
 
         def transpose_pairs(what, index):
             pairs = loaded[(what, index)][:].bitcast(F32)
@@ -207,9 +216,13 @@ def tile_modelnew_pb_kernel(
                 bank = psum.tile([P, BANK], F32, tag="bank")
                 for m in range(4):
                     run, u = 2 * h + m // 2, m % 2
+                    if ("apart", what, index) in live:
+                        taken = live[("apart", what, index)][:, run, u, :]
+                    else:
+                        taken = pairs[:, 2 * P * run + u : 2 * P * (run + 1) : 2]
                     nc.tensor.transpose(
                         out=bank[:, m * P : (m + 1) * P],
-                        in_=pairs[:, 2 * P * run + u : 2 * P * (run + 1) : 2],
+                        in_=taken,
                         identity=ident_f32[:],
                     )
                 live[("bank", what, index, h)] = bank
@@ -297,15 +310,14 @@ def tile_modelnew_pb_kernel(
             nc.scalar.activation(
                 out=squares[:], in_=live[("ckv", j)][:], func=ACT.Square, accum_out=sum_squares[:]
             )
-            rms = work.tile([P, 1], F32, tag="rms")
-            nc.scalar.activation(
-                out=rms[:], in_=sum_squares[:], func=ACT.Sqrt, bias=eps[:], scale=1.0 / LATENT
-            )
-            live[("rms", j)] = rms
-
-        def invert(j):
             inverse = work.tile([P, 1], F32, tag="inverse")
-            nc.vector.reciprocal(out=inverse[:], in_=live[("rms", j)][:])
+            nc.scalar.activation(
+                out=inverse[:],
+                in_=sum_squares[:],
+                func=ACT.Abs_reciprocal_sqrt,
+                bias=eps[:],
+                scale=1.0 / LATENT,
+            )
             live[("inverse", j)] = inverse
 
         def normalise(j):
@@ -346,27 +358,31 @@ def tile_modelnew_pb_kernel(
             sin = sin_cos[:, 0]
             cos = sin_cos[:, 1]
             by_cos = const.tile([P, TILES, ROPE], F32)
-            nc.vector.tensor_tensor(
+            nc.gpsimd.tensor_tensor(
                 out=by_cos[:].rearrange("p j (h f) -> p j h f", h=2),
                 in0=kpe[:].rearrange("p j (h f) -> p j h f", h=2),
                 in1=cos.unsqueeze(2).to_broadcast([P, TILES, 2, half]),
                 op=ALU.mult,
             )
             by_sin = const.tile([P, TILES, ROPE], F32)
-            nc.vector.scalar_tensor_tensor(
-                out=by_sin[:, :, 0:half],
-                in0=kpe[:, :, half:ROPE],
-                scalar=-1.0,
-                in1=sin,
-                op0=ALU.mult,
-                op1=ALU.mult,
-            )
-            nc.vector.tensor_tensor(
-                out=by_sin[:, :, half:ROPE], in0=kpe[:, :, 0:half], in1=sin, op=ALU.mult
+            nc.gpsimd.tensor_tensor(
+                out=by_sin[:].rearrange("p j (h f) -> p j h f", h=2),
+                in0=kpe[:].rearrange("p j (h f) -> p j h f", h=2),
+                in1=sin.unsqueeze(2).to_broadcast([P, TILES, 2, half]),
+                op=ALU.mult,
             )
             rotated = const.tile([P, TILES, ROPE], F32)
-            nc.vector.tensor_tensor(
-                out=rotated[:], in0=by_cos[:], in1=by_sin[:], op=ALU.add
+            nc.gpsimd.tensor_tensor(
+                out=rotated[:, :, 0:half],
+                in0=by_cos[:, :, 0:half],
+                in1=by_sin[:, :, half:ROPE],
+                op=ALU.subtract,
+            )
+            nc.gpsimd.tensor_tensor(
+                out=rotated[:, :, half:ROPE],
+                in0=by_cos[:, :, half:ROPE],
+                in1=by_sin[:, :, 0:half],
+                op=ALU.add,
             )
             live["rotated"] = rotated
 
@@ -420,12 +436,15 @@ def tile_modelnew_pb_kernel(
                 )
 
         keep_clock_up(4)
+        rotate()
         transpose_pairs("wa", 0)
         regroup("wa", 0, 0, on_vector)
         regroup("wa", 0, 1, on_vector)
         transpose_pairs("wa", 1)
         regroup("wa", 1, 0, on_scalar)
         regroup("wa", 1, 1, on_vector)
+        spread_gain()
+        order_gain()
         transpose_pairs("wa", 2)
         regroup("wa", 2, 0, on_scalar)
         quantise("wa", 0)
@@ -442,59 +461,62 @@ def tile_modelnew_pb_kernel(
         regroup("x", 1, 0, on_scalar)
         regroup("x", 1, 1, on_scalar)
         transpose_pairs("x", 2)
+        separate("x", 3)
         quantise("x", 1)
         regroup("x", 2, 0, on_scalar)
-        regroup("x", 2, 1, on_vector)
+        regroup("x", 2, 1, on_scalar)
+        first_matmul(0)
         transpose_pairs("x", 3)
-        regroup("x", 3, 0, on_scalar)
+        root_mean_square(0)
         quantise("x", 2)
+        regroup("x", 3, 0, on_scalar)
+        first_matmul(1)
+        normalise(0)
+        separate("wb", 0)
         regroup("x", 3, 1, on_scalar)
-        spread_gain()
-        order_gain()
+        first_matmul(2)
+        root_mean_square(1)
         quantise("x", 3)
-        for j in range(TILES):
-            first_matmul(j)
-        rotate()
-        fill_rotated(0)
-        for j in range(TILES):
-            root_mean_square(j)
-            invert(j)
-            normalise(j)
-        transpose_normed(0)
-        transpose_normed(1)
-        regroup_normed(0, on_scalar)
         transpose_pairs("wb", 0)
-        regroup_normed(1, on_scalar)
-        quantise_normed(0)
-        transpose_normed(2)
-        transpose_normed(3)
-        regroup_bank(0, 0, on_scalar)
-        quantise_normed(1)
+        transpose_normed(0)
+        normalise(1)
+        fill_rotated(0)
+        root_mean_square(2)
         regroup_bank(0, 1, on_vector)
-        regroup_normed(2, on_scalar)
-        transpose_pairs("wb", 1)
+        regroup_bank(0, 0, on_scalar)
+        first_matmul(3)
+        normalise(2)
+        regroup_normed(0, on_scalar)
         quantise("wb", 0)
-        regroup_normed(3, on_scalar)
-        quantise_normed(2)
+        transpose_normed(1)
+        transpose_normed(2)
+        root_mean_square(3)
+        quantise_normed(0)
+        regroup_normed(1, on_scalar)
+        transpose_pairs("wb", 1)
+        normalise(3)
+        regroup_normed(2, on_scalar)
+        quantise_normed(1)
         second_matmul(0, 0)
+        transpose_normed(3)
         second_matmul(0, 1)
-        quantise_normed(3)
         regroup_bank(1, 0, on_scalar)
+        quantise_normed(2)
         copy_out(0, 0, on_vector)
-        second_matmul(0, 2)
-        second_matmul(0, 3)
+        regroup_normed(3, on_scalar)
         copy_out(0, 1, on_scalar)
         store(0, 0, 2)
+        second_matmul(0, 2)
         regroup_bank(1, 1, on_vector)
+        quantise_normed(3)
         copy_out(0, 2, on_scalar)
+        transpose_pairs("wb", 2)
+        second_matmul(0, 3)
+        quantise("wb", 1)
         copy_out(0, 3, on_vector)
         store(0, 2, 4)
-        quantise("wb", 1)
-        fill_rotated(1)
-        transpose_pairs("wb", 2)
         regroup_rows(2, on_scalar)
-        fill_rotated(2)
-        fill_rotated(3)
+        fill_rotated(1)
 
         for c in range(1, PAIRS):
             for j in range(TILES):
@@ -508,5 +530,7 @@ def tile_modelnew_pb_kernel(
             copy_out(c, 2, on_vector)
             copy_out(c, 3, on_scalar)
             store(c, 0, TILES)
+            if c in (1, 2):
+                fill_rotated(c + 1)
             if c + 2 < PAIRS:
                 regroup_rows(c + 2, on_scalar)

@@ -31,7 +31,6 @@ HEAD_OUT = 2 * HEAD_KEY
 SPLIT_PAIRS = 2
 EPS = 1e-6
 THETA = 10000.0
-WARM_START = 9
 FLOPS = 2 * BATCH * 256 * D_MODEL * LATENT + 2 * BATCH * 256 * LATENT * HEADS * 2 * NOPE
 
 
@@ -57,15 +56,12 @@ def tile_modelnew_pb_kernel(
                 out=kpe[b:P:BATCH, :, :],
                 in_=k_pe_raw[b].rearrange("(q j) d -> q j d", j=TILES),
             )
-        gain_row = const.tile([P, LATENT], BF16)
-        nc.vector.memset(gain_row[:].bitcast(F32), 0.0)
-        nc.scalar.dma_start(
-            out=gain_row[0:1, :], in_=kv_a_ln_w.rearrange("(o n) -> o n", o=1)
-        )
         ones = const.tile([P, P], BF16)
         nc.vector.memset(ones[:], 1.0)
+        gain_row = const.tile([P, LATENT], BF16)
+        nc.vector.memset(gain_row[:].bitcast(F32), 0.0)
         zeros = const.tile([P, BANK], BF16)
-        nc.vector.memset(zeros[:].bitcast(F32), 0.0)
+        nc.gpsimd.memset(zeros[:].bitcast(F32), 0.0)
         twice_p = const.tile([P, TILES], I32)
         nc.gpsimd.iota(out=twice_p[:], pattern=[[0, TILES]], base=0, channel_multiplier=2)
         j_index = const.tile([P, TILES], I32)
@@ -74,14 +70,15 @@ def tile_modelnew_pb_kernel(
         nc.scalar.activation(out=sin_first[:], in_=ones[:, 0:1], func=ACT.Sin)
 
         loaded = {}
-        wa_view = kv_a_w_ckv.rearrange("(p t) k -> t p k", t=4)
+        wa_view = kv_a_w_ckv.rearrange("(h q u e) k -> u h e q k", h=2, u=2, e=2)
         x_view = hidden_states.rearrange("b (q j) k -> b j q k", j=TILES)
         wb_view = kv_b_w.rearrange("(c p i) k -> c p (i k)", c=PAIRS, i=4)
 
         def load(what, index):
             tile = raw.tile([P, D_MODEL], BF16, name="%s_raw%d" % (what, index))
             if what == "wa":
-                nc.sync.dma_start(out=tile[:], in_=wa_view[index])
+                for e in range(2):
+                    nc.sync.dma_start(out=tile[e:P:2, :], in_=wa_view[index // 2, index % 2, e])
             elif what == "x":
                 for b in range(BATCH):
                     nc.sync.dma_start(out=tile[b:P:BATCH, :], in_=x_view[b, index])
@@ -89,7 +86,11 @@ def tile_modelnew_pb_kernel(
                 nc.sync.dma_start(out=tile[:], in_=wb_view[index])
             loaded[(what, index)] = tile
 
-        for t in range(4):
+        load("wa", 0)
+        nc.sync.dma_start(
+            out=gain_row[0:1, :], in_=kv_a_ln_w.rearrange("(o n) -> o n", o=1)
+        )
+        for t in range(1, 4):
             load("wa", t)
         for j in range(TILES):
             load("x", j)
@@ -98,8 +99,6 @@ def tile_modelnew_pb_kernel(
 
         ident_f32 = const.tile([P, P], F32)
         make_identity(nc, ident_f32[:])
-        ident_bf16 = const.tile([P, P], BF16)
-        make_identity(nc, ident_bf16[:])
         eps = const.tile([P, 1], F32)
         nc.gpsimd.memset(eps[:], EPS)
 
@@ -180,13 +179,11 @@ def tile_modelnew_pb_kernel(
         def on_scalar(out, in_):
             nc.scalar.copy(out=out, in_=in_)
 
-        def keep_clock_up(count, columns=BANK):
-            if "dummy" not in live:
-                dummy = psum.tile([P, BANK], F32, tag="bank")
-                live["dummy"] = dummy
+        def keep_clock_up(count):
+            dummy = psum.tile([P, BANK], F32, tag="bank")
             for repeat in range(count):
                 nc.tensor.matmul(
-                    out=live["dummy"][:, 0:columns], lhsT=ones[:], rhs=zeros[:, 0:columns], start=True, stop=True
+                    out=dummy[:], lhsT=ones[:], rhs=zeros[:], start=True, stop=True
                 )
 
         def spread_gain():
@@ -198,8 +195,8 @@ def tile_modelnew_pb_kernel(
 
         def order_gain():
             nc.vector.tensor_copy(
-                out=gain_all[:].rearrange("q (t p) -> q t p", t=4),
-                in_=live["gain"][:].rearrange("q (p t) -> q t p", t=4),
+                out=gain_all[:].rearrange("q (u p e) -> q u p e", u=2, e=2),
+                in_=live["gain"][:].rearrange("q (p u e) -> q u p e", u=2, e=2),
             )
 
         def separate(what, index):
@@ -333,25 +330,29 @@ def tile_modelnew_pb_kernel(
             live[("normed", j)] = normed
 
         def transpose_normed(j):
-            bank = psum.tile([P, 4, P], BF16, tag="bank")
-            for t in range(4):
+            bank = psum.tile([P, 2, P], F32, tag="bank")
+            pairs = live[("normed", j)][:].bitcast(F32)
+            for u in range(2):
                 nc.tensor.transpose(
-                    out=bank[:, t, :],
-                    in_=live[("normed", j)][:, t * P : (t + 1) * P],
-                    identity=ident_bf16[:],
+                    out=bank[:, u, :],
+                    in_=pairs[:, u * P : (u + 1) * P],
+                    identity=ident_f32[:],
                 )
             live[("bank", "normed", j)] = bank
 
         def regroup_normed(j, copy):
-            grouped = work.tile([P, P, 4], BF16, tag="grouped_normed", align_bytes=64)
-            copy(grouped[:], live[("bank", "normed", j)][:].rearrange("q t r -> q r t"))
+            grouped = work.tile([P, 4 * P], BF16, tag="grouped_normed", align_bytes=64)
+            copy(
+                grouped[:].bitcast(F32).rearrange("q (r u) -> q r u", u=2),
+                live[("bank", "normed", j)][:].rearrange("q u r -> q r u"),
+            )
             live[("grouped", "normed", j)] = grouped
 
         def quantise_normed(j):
             nc.vector.quantize_mx(
                 out=n_codes[:, j, :].bitcast(FP8X4),
                 scales=n_scales[:, j, :],
-                in_=live[("grouped", "normed", j)][:].rearrange("q r t -> q (r t)"),
+                in_=live[("grouped", "normed", j)][:],
             )
 
         def rotate():
@@ -435,7 +436,7 @@ def tile_modelnew_pb_kernel(
                     in_=live[("value", c)][b:P:BATCH, :, j0:j1, :],
                 )
 
-        keep_clock_up(4)
+        keep_clock_up(5)
         rotate()
         transpose_pairs("wa", 0)
         regroup("wa", 0, 0, on_vector)
@@ -469,6 +470,8 @@ def tile_modelnew_pb_kernel(
         transpose_pairs("x", 3)
         root_mean_square(0)
         quantise("x", 2)
+        fill_rotated(0)
+        fill_rotated(1)
         regroup("x", 3, 0, on_scalar)
         first_matmul(1)
         normalise(0)
@@ -480,12 +483,11 @@ def tile_modelnew_pb_kernel(
         transpose_pairs("wb", 0)
         transpose_normed(0)
         normalise(1)
-        fill_rotated(0)
         root_mean_square(2)
-        regroup_bank(0, 1, on_vector)
         regroup_bank(0, 0, on_scalar)
         first_matmul(3)
         normalise(2)
+        regroup_bank(0, 1, on_vector)
         regroup_normed(0, on_scalar)
         quantise("wb", 0)
         transpose_normed(1)
@@ -516,7 +518,6 @@ def tile_modelnew_pb_kernel(
         copy_out(0, 3, on_vector)
         store(0, 2, 4)
         regroup_rows(2, on_scalar)
-        fill_rotated(1)
 
         for c in range(1, PAIRS):
             for j in range(TILES):
@@ -525,9 +526,9 @@ def tile_modelnew_pb_kernel(
                 transpose_pairs("wb", c + 2)
             copy_out(c, 0, on_vector)
             copy_out(c, 1, on_scalar)
+            copy_out(c, 2, on_vector)
             if c + 1 < PAIRS:
                 quantise("wb", c + 1)
-            copy_out(c, 2, on_vector)
             copy_out(c, 3, on_scalar)
             store(c, 0, TILES)
             if c in (1, 2):

import math
from contextlib import ExitStack

import concourse.mybir as mybir
from concourse.masks import make_identity

F32 = mybir.dt.float32
BF16 = mybir.dt.bfloat16
I32 = mybir.dt.int32
U32 = mybir.dt.uint32
U8 = mybir.dt.uint8
FP8X4 = mybir.dt.float8_e4m3fn_x4
ALU = mybir.AluOpType
ACT = mybir.ActivationFunctionType

P = 128
BATCH = 2
D_MODEL = 2048
LATENT = 512
HEADS = 16
NOPE = 128
ROPE = 64
K_PASS = 512
PASSES = D_MODEL // K_PASS
BANK = 512
TILES = 4
PAIRS = HEADS // 2
OUT_TILES = 4
HEAD_KEY = TILES * (NOPE + ROPE)
HEAD_OUT = 2 * HEAD_KEY
SPLIT_PAIRS = 2
EPS = 1e-6
THETA = 10000.0
FLOPS = 2 * BATCH * 256 * D_MODEL * LATENT + 2 * BATCH * 256 * LATENT * HEADS * 2 * NOPE


def tile_modelnew_pb_kernel(
    tc, hidden_states, kv_a_w_ckv, k_pe_raw, kv_a_ln_w, kv_b_w, out_0, out_1
):
    nc = tc.nc
    with ExitStack() as ctx:
        ctx.enter_context(tc.manual_schedule())
        const = ctx.enter_context(tc.tile_pool(name="const", bufs=1))
        raw = ctx.enter_context(tc.tile_pool(name="raw", bufs=1))
        keep = ctx.enter_context(tc.tile_pool(name="keep", bufs=1))
        outs = ctx.enter_context(tc.tile_pool(name="outs", bufs=1))
        grp = ctx.enter_context(tc.tile_pool(name="grp", bufs=4))
        sep = ctx.enter_context(tc.tile_pool(name="sep", bufs=3))
        wa_grp = ctx.enter_context(tc.tile_pool(name="wa_grp", bufs=2))
        work = ctx.enter_context(tc.tile_pool(name="work", bufs=TILES))
        psum = ctx.enter_context(tc.psum_pool(name="psum", bufs=8))

        kpe = const.tile([P, TILES, ROPE], BF16)
        for b in range(BATCH):
            nc.scalar.dma_start(
                out=kpe[b:P:BATCH, :, :],
                in_=k_pe_raw[b].rearrange("(q j) d -> q j d", j=TILES),
            )
        ones = const.tile([P, P], BF16)
        nc.vector.memset(ones[:], 1.0)
        gain_row = const.tile([P, LATENT], BF16)
        nc.vector.memset(gain_row[:].bitcast(F32), 0.0)
        zeros = const.tile([P, BANK], BF16)
        nc.gpsimd.memset(zeros[:].bitcast(F32), 0.0)
        twice_p = const.tile([P, TILES], I32)
        nc.gpsimd.iota(out=twice_p[:], pattern=[[0, TILES]], base=0, channel_multiplier=2)
        j_index = const.tile([P, TILES], I32)
        nc.gpsimd.iota(out=j_index[:], pattern=[[1, TILES]], base=0, channel_multiplier=0)
        sin_first = const.tile([P, 1], F32)
        nc.scalar.activation(out=sin_first[:], in_=ones[:, 0:1], func=ACT.Sin)

        loaded = {}
        wa_view = kv_a_w_ckv.rearrange("(h q u e) k -> u h e q k", h=2, u=2, e=2)
        x_view = hidden_states.rearrange("b (q j) k -> b j q k", j=TILES)
        wb_view = kv_b_w.rearrange("(c p i) k -> c p (i k)", c=PAIRS, i=4)

        def load(what, index):
            tile = raw.tile([P, D_MODEL], BF16, name="%s_raw%d" % (what, index))
            if what == "wa":
                for e in range(2):
                    nc.sync.dma_start(out=tile[e:P:2, :], in_=wa_view[index // 2, index % 2, e])
            elif what == "x":
                for b in range(BATCH):
                    nc.sync.dma_start(out=tile[b:P:BATCH, :], in_=x_view[b, index])
            else:
                nc.sync.dma_start(out=tile[:], in_=wb_view[index])
            loaded[(what, index)] = tile

        load("wa", 0)
        nc.sync.dma_start(
            out=gain_row[0:1, :], in_=kv_a_ln_w.rearrange("(o n) -> o n", o=1)
        )
        for t in range(1, 4):
            load("wa", t)
        for j in range(TILES):
            load("x", j)
        for c in range(PAIRS):
            load("wb", c)

        ident_f32 = const.tile([P, P], F32)
        make_identity(nc, ident_f32[:])
        eps = const.tile([P, 1], F32)
        nc.gpsimd.memset(eps[:], EPS)

        half = ROPE // 2
        ratio = THETA ** (-2.0 / ROPE)
        freq = const.tile([P, half], F32)
        nc.vector.tensor_scalar(
            out=freq[:, 0:1],
            in0=ones[:, 0:1],
            scalar1=1.0 / (2.0 * math.pi),
            scalar2=None,
            op0=ALU.mult,
        )
        four_q = const.tile([P, TILES], I32)
        nc.vector.tensor_single_scalar(
            out=four_q[:], in_=twice_p[:], scalar=0x1FC, op=ALU.bitwise_and
        )
        for width, copies in ((1, 4), (4, 4), (16, 2)):
            for r in range(1, copies):
                nc.vector.tensor_scalar(
                    out=freq[:, r * width : (r + 1) * width],
                    in0=freq[:, 0:width],
                    scalar1=ratio ** (r * width),
                    scalar2=None,
                    op0=ALU.mult,
                )
        position = const.tile([P, TILES], F32)
        nc.vector.tensor_tensor(
            out=position[:], in0=four_q[:], in1=j_index[:], op=ALU.add
        )
        turns = const.tile([P, 2, TILES, half], F32)
        nc.vector.tensor_tensor(
            out=turns[:, 0],
            in0=position[:].unsqueeze(2).to_broadcast([P, TILES, half]),
            in1=freq[:].unsqueeze(1).to_broadcast([P, TILES, half]),
            op=ALU.mult,
        )
        nc.vector.tensor_scalar(
            out=turns[:, 1], in0=turns[:, 0], scalar1=0.25, scalar2=None, op0=ALU.add
        )
        n_table = 2 * TILES * half
        turns_flat = turns[:].rearrange("p c j f -> p (c j f)")
        whole = const.tile([P, n_table], I32)
        nc.vector.tensor_copy(out=whole[:], in_=turns_flat)
        remainder = const.tile([P, n_table], F32)
        nc.vector.tensor_tensor(
            out=remainder[:], in0=turns_flat, in1=whole[:], op=ALU.subtract
        )
        sin_cos = const.tile([P, 2, TILES, ROPE // 2], F32)
        nc.scalar.activation(
            out=sin_cos[:].rearrange("p c j f -> p (c j f)"),
            in_=remainder[:],
            func=ACT.Sin,
            scale=2.0 * math.pi,
        )

        sqrt_early = const.tile([P, 1], F32)
        nc.scalar.activation(out=sqrt_early[:], in_=eps[:], func=ACT.Abs_reciprocal_sqrt)

        wa_codes = keep.tile([P, 2, PASSES, 2 * P], U32, align_bytes=64)
        wa_scales = keep.tile([P, 2, PASSES, 2 * P], U8, align_bytes=64)
        x_codes = keep.tile([P, TILES, PASSES, P], U32, align_bytes=64)
        x_scales = keep.tile([P, TILES, PASSES, P], U8, align_bytes=64)
        n_codes = keep.tile([P, TILES, P], U32, align_bytes=64)
        n_scales = keep.tile([P, TILES, P], U8, align_bytes=64)
        wb_codes = keep.tile([P, PAIRS, BANK], U32, align_bytes=64)
        wb_scales = keep.tile([P, PAIRS, BANK], U8, align_bytes=64)

        gain_all = const.tile([P, LATENT], F32)
        key_view = out_0.rearrange("b h (q j) d -> b q h j d", j=TILES)
        value_view = out_1.rearrange("b h (q j) d -> b q h j d", j=TILES)

        live = {}

        def on_vector(out, in_):
            nc.vector.tensor_copy(out=out, in_=in_)

        def on_scalar(out, in_):
            nc.scalar.copy(out=out, in_=in_)

        def keep_clock_up(count):
            dummy = psum.tile([P, BANK], F32, tag="bank")
            for repeat in range(count):
                nc.tensor.matmul(
                    out=dummy[:], lhsT=ones[:], rhs=zeros[:], start=True, stop=True
                )

        def spread_gain():
            gain_bank = psum.tile([P, LATENT], F32, tag="bank")
            nc.tensor.matmul(
                out=gain_bank[:], lhsT=ones[:], rhs=gain_row[:], start=True, stop=True
            )
            live["gain"] = gain_bank

        def order_gain():
            nc.vector.tensor_copy(
                out=gain_all[:].rearrange("q (u p e) -> q u p e", u=2, e=2),
                in_=live["gain"][:].rearrange("q (p u e) -> q u p e", u=2, e=2),
            )

        def separate(what, index):
            apart = sep.tile([P, 4, 2, P], F32, tag="apart")
            nc.vector.tensor_copy(
                out=apart[:],
                in_=loaded[(what, index)][:].bitcast(F32).rearrange("p (n q u) -> p n u q", n=4, u=2),
            )
            live[("apart", what, index)] = apart

        def transpose_pairs(what, index):
            pairs = loaded[(what, index)][:].bitcast(F32)
            for h in range(2):
                bank = psum.tile([P, BANK], F32, tag="bank")
                for m in range(4):
                    run, u = 2 * h + m // 2, m % 2
                    if ("apart", what, index) in live:
                        taken = live[("apart", what, index)][:, run, u, :]
                    else:
                        taken = pairs[:, 2 * P * run + u : 2 * P * (run + 1) : 2]
                    nc.tensor.transpose(
                        out=bank[:, m * P : (m + 1) * P],
                        in_=taken,
                        identity=ident_f32[:],
                    )
                live[("bank", what, index, h)] = bank

        def grouped_tile(what, index):
            if ("grouped", what, index) not in live:
                if what == "wa":
                    grouped = wa_grp.tile([P, 8 * BANK], BF16, tag="grouped_wa", align_bytes=64)
                else:
                    grouped = grp.tile([P, 4 * BANK], BF16, tag="grouped", align_bytes=64)
                live[("grouped", what, index)] = grouped
            return live[("grouped", what, index)]

        def regroup(what, index, h, copy):
            if what == "wa":
                rows = slice((index % 2) * P, (index % 2 + 1) * P)
                grouped = grouped_tile(what, index // 2)
            else:
                rows = slice(0, P)
                grouped = grouped_tile(what, index)
            view = (
                grouped[:].bitcast(F32).rearrange("q (g r u) -> q g r u", g=PASSES, u=2)
            )[:, :, rows, :]
            copy(
                view[:, 2 * h : 2 * h + 2],
                live[("bank", what, index, h)][:].rearrange("q (g u r) -> q g r u", g=2, u=2),
            )

        def regroup_rows(c, copy):
            view = (
                grouped_tile("wb", c)[:]
                .bitcast(F32)
                .rearrange("q (p a m) -> q a p m", a=2, m=4)
            )
            for a in range(2):
                copy(view[:, a], live[("bank", "wb", c, a)][:].rearrange("q (m p) -> q p m", m=4))

        def regroup_bank(c, a, copy):
            view = (
                grouped_tile("wb", c)[:]
                .bitcast(F32)
                .rearrange("q (p a m) -> q a p m", a=2, m=4)
            )
            copy(view[:, a], live[("bank", "wb", c, a)][:].rearrange("q (m p) -> q p m", m=4))

        def quantise(what, index):
            grouped = live[("grouped", what, index)]
            if what == "wa":
                nc.vector.quantize_mx(
                    out=wa_codes[:, index].rearrange("q g r -> q (g r)").bitcast(FP8X4),
                    scales=wa_scales[:, index].rearrange("q g r -> q (g r)"),
                    in_=grouped[:],
                )
            elif what == "x":
                nc.vector.quantize_mx(
                    out=x_codes[:, index].rearrange("q g r -> q (g r)").bitcast(FP8X4),
                    scales=x_scales[:, index].rearrange("q g r -> q (g r)"),
                    in_=grouped[:],
                )
            else:
                nc.vector.quantize_mx(
                    out=wb_codes[:, index, :].bitcast(FP8X4),
                    scales=wb_scales[:, index, :],
                    in_=grouped[:],
                )

        def first_matmul(j):
            ckv = psum.tile([P, LATENT], F32, tag="bank")
            for half in range(2):
                for g in range(PASSES):
                    nc.tensor.matmul_mx(
                        out=ckv[:, half * 2 * P : (half + 1) * 2 * P],
                        lhsT=x_codes[:, j, g, :].bitcast(FP8X4),
                        lhsT_scale=x_scales[:, j, g, :],
                        rhs=wa_codes[:, half, g, :].bitcast(FP8X4),
                        rhs_scale=wa_scales[:, half, g, :],
                        start=(g == 0),
                        stop=(g == PASSES - 1),
                    )
            live[("ckv", j)] = ckv

        def root_mean_square(j):
            squares = work.tile([P, LATENT], BF16, tag="squares")
            sum_squares = work.tile([P, 1], F32, tag="sum_squares")
            nc.scalar.activation(
                out=squares[:], in_=live[("ckv", j)][:], func=ACT.Square, accum_out=sum_squares[:]
            )
            inverse = work.tile([P, 1], F32, tag="inverse")
            nc.scalar.activation(
                out=inverse[:],
                in_=sum_squares[:],
                func=ACT.Abs_reciprocal_sqrt,
                bias=eps[:],
                scale=1.0 / LATENT,
            )
            live[("inverse", j)] = inverse

        def normalise(j):
            normed = work.tile([P, LATENT], BF16, tag="normed")
            nc.vector.scalar_tensor_tensor(
                out=normed[:],
                in0=live[("ckv", j)][:],
                scalar=live[("inverse", j)][:],
                in1=gain_all[:],
                op0=ALU.mult,
                op1=ALU.mult,
            )
            live[("normed", j)] = normed

        def transpose_normed(j):
            bank = psum.tile([P, 2, P], F32, tag="bank")
            pairs = live[("normed", j)][:].bitcast(F32)
            for u in range(2):
                nc.tensor.transpose(
                    out=bank[:, u, :],
                    in_=pairs[:, u * P : (u + 1) * P],
                    identity=ident_f32[:],
                )
            live[("bank", "normed", j)] = bank

        def regroup_normed(j, copy):
            grouped = work.tile([P, 4 * P], BF16, tag="grouped_normed", align_bytes=64)
            copy(
                grouped[:].bitcast(F32).rearrange("q (r u) -> q r u", u=2),
                live[("bank", "normed", j)][:].rearrange("q u r -> q r u"),
            )
            live[("grouped", "normed", j)] = grouped

        def quantise_normed(j):
            nc.vector.quantize_mx(
                out=n_codes[:, j, :].bitcast(FP8X4),
                scales=n_scales[:, j, :],
                in_=live[("grouped", "normed", j)][:],
            )

        def rotate():
            sin = sin_cos[:, 0]
            cos = sin_cos[:, 1]
            by_cos = const.tile([P, TILES, ROPE], F32)
            nc.gpsimd.tensor_tensor(
                out=by_cos[:].rearrange("p j (h f) -> p j h f", h=2),
                in0=kpe[:].rearrange("p j (h f) -> p j h f", h=2),
                in1=cos.unsqueeze(2).to_broadcast([P, TILES, 2, half]),
                op=ALU.mult,
            )
            by_sin = const.tile([P, TILES, ROPE], F32)
            nc.gpsimd.tensor_tensor(
                out=by_sin[:].rearrange("p j (h f) -> p j h f", h=2),
                in0=kpe[:].rearrange("p j (h f) -> p j h f", h=2),
                in1=sin.unsqueeze(2).to_broadcast([P, TILES, 2, half]),
                op=ALU.mult,
            )
            rotated = const.tile([P, TILES, ROPE], F32)
            nc.gpsimd.tensor_tensor(
                out=rotated[:, :, 0:half],
                in0=by_cos[:, :, 0:half],
                in1=by_sin[:, :, half:ROPE],
                op=ALU.subtract,
            )
            nc.gpsimd.tensor_tensor(
                out=rotated[:, :, half:ROPE],
                in0=by_cos[:, :, half:ROPE],
                in1=by_sin[:, :, 0:half],
                op=ALU.add,
            )
            live["rotated"] = rotated

        def fill_rotated(c):
            last = (TILES - 1) * (NOPE + ROPE)
            both = outs.tile([P, 2 * HEAD_OUT + last], F32, name="out%d" % c)
            heads = both[:, 0 : 2 * HEAD_OUT].rearrange("p (h y) -> p h y", h=2)
            key = heads[:, :, 0:HEAD_KEY].rearrange("p h (j d) -> p h j d", j=TILES)
            value = heads[:, :, HEAD_KEY : HEAD_KEY + TILES * NOPE].rearrange("p h (j d) -> p h j d", j=TILES)
            nc.vector.tensor_copy(
                out=key[:, :, :, NOPE : NOPE + ROPE],
                in_=live["rotated"][:].unsqueeze(1).to_broadcast([P, 2, TILES, ROPE]),
            )
            for pair in range(c, PAIRS, OUT_TILES):
                live[("both", pair)] = both
                live[("key", pair)] = key
                live[("value", pair)] = value

        def second_matmul(c, j):
            kv = psum.tile([P, BANK], F32, tag="bank")
            nc.tensor.matmul_mx(
                out=kv[:],
                lhsT=n_codes[:, j, :].bitcast(FP8X4),
                lhsT_scale=n_scales[:, j, :],
                rhs=wb_codes[:, c, :].bitcast(FP8X4),
                rhs_scale=wb_scales[:, c, :],
                start=True,
                stop=True,
            )
            live[("kv", c, j)] = kv

        def copy_out(c, j, copy):
            parts = live[("kv", c, j)][:].rearrange("p (h s d) -> p h s d", h=2, s=2)
            first = j * (NOPE + ROPE)
            apart = HEAD_KEY + j * NOPE - first
            view = live[("both", c)][:, first : first + 2 * HEAD_OUT]
            view = view.rearrange("p (h y) -> p h y", h=2)[:, :, 0 : 2 * apart]
            view = view.rearrange("p h (s x) -> p h s x", s=2)[:, :, :, 0:NOPE]
            copy(view, parts)

        def store(c, j0, j1):
            heads = slice(2 * c, 2 * c + 2)
            for b in range(BATCH):
                nc.sync.dma_start(
                    out=key_view[b, :, heads, j0:j1, :],
                    in_=live[("key", c)][b:P:BATCH, :, j0:j1, :],
                )
                nc.sync.dma_start(
                    out=value_view[b, :, heads, j0:j1, :],
                    in_=live[("value", c)][b:P:BATCH, :, j0:j1, :],
                )

        keep_clock_up(5)
        rotate()
        transpose_pairs("wa", 0)
        regroup("wa", 0, 0, on_vector)
        regroup("wa", 0, 1, on_vector)
        transpose_pairs("wa", 1)
        regroup("wa", 1, 0, on_scalar)
        regroup("wa", 1, 1, on_vector)
        spread_gain()
        order_gain()
        transpose_pairs("wa", 2)
        regroup("wa", 2, 0, on_scalar)
        quantise("wa", 0)
        regroup("wa", 2, 1, on_scalar)
        transpose_pairs("wa", 3)
        regroup("wa", 3, 0, on_scalar)
        regroup("wa", 3, 1, on_vector)
        transpose_pairs("x", 0)
        regroup("x", 0, 0, on_scalar)
        quantise("wa", 1)
        regroup("x", 0, 1, on_scalar)
        transpose_pairs("x", 1)
        quantise("x", 0)
        regroup("x", 1, 0, on_scalar)
        regroup("x", 1, 1, on_scalar)
        transpose_pairs("x", 2)
        separate("x", 3)
        quantise("x", 1)
        regroup("x", 2, 0, on_scalar)
        regroup("x", 2, 1, on_scalar)
        first_matmul(0)
        transpose_pairs("x", 3)
        root_mean_square(0)
        quantise("x", 2)
        fill_rotated(0)
        fill_rotated(1)
        regroup("x", 3, 0, on_scalar)
        first_matmul(1)
        normalise(0)
        separate("wb", 0)
        regroup("x", 3, 1, on_scalar)
        first_matmul(2)
        root_mean_square(1)
        quantise("x", 3)
        transpose_pairs("wb", 0)
        transpose_normed(0)
        normalise(1)
        root_mean_square(2)
        regroup_bank(0, 0, on_scalar)
        first_matmul(3)
        normalise(2)
        regroup_bank(0, 1, on_vector)
        regroup_normed(0, on_scalar)
        quantise("wb", 0)
        transpose_normed(1)
        transpose_normed(2)
        root_mean_square(3)
        quantise_normed(0)
        regroup_normed(1, on_scalar)
        transpose_pairs("wb", 1)
        normalise(3)
        regroup_normed(2, on_scalar)
        quantise_normed(1)
        second_matmul(0, 0)
        transpose_normed(3)
        second_matmul(0, 1)
        regroup_bank(1, 0, on_scalar)
        quantise_normed(2)
        copy_out(0, 0, on_vector)
        regroup_normed(3, on_scalar)
        copy_out(0, 1, on_scalar)
        store(0, 0, 2)
        second_matmul(0, 2)
        regroup_bank(1, 1, on_vector)
        quantise_normed(3)
        copy_out(0, 2, on_scalar)
        transpose_pairs("wb", 2)
        second_matmul(0, 3)
        quantise("wb", 1)
        copy_out(0, 3, on_vector)
        store(0, 2, 4)
        regroup_rows(2, on_scalar)

        for c in range(1, PAIRS):
            for j in range(TILES):
                second_matmul(c, j)
            if c + 2 < PAIRS:
                transpose_pairs("wb", c + 2)
            copy_out(c, 0, on_vector)
            copy_out(c, 1, on_scalar)
            copy_out(c, 2, on_vector)
            if c + 1 < PAIRS:
                quantise("wb", c + 1)
            copy_out(c, 3, on_scalar)
            store(c, 0, TILES)
            if c in (1, 2):
                fill_rotated(c + 1)
            if c + 2 < PAIRS:
                regroup_rows(c + 2, on_scalar)
